import numpy as np
import ml_dtypes


def mxq(x, axis, fmt="e4m3"):
    dtype, down = {"e4m3": (ml_dtypes.float8_e4m3fn, 7), "e5m2": (ml_dtypes.float8_e5m2, 14)}[fmt]
    v = np.moveaxis(np.asarray(x, np.float32).astype(ml_dtypes.bfloat16).astype(np.float64), axis, -1)
    blocks = v.reshape(v.shape[:-1] + (-1, 32))
    amax = np.abs(blocks).max(-1, keepdims=True)
    byte = np.maximum(np.where(amax > 0, np.frexp(amax)[1] - 1 + 127, 0) - down, 1)
    scale = np.exp2(byte - 127.0)
    codes = (blocks / scale).astype(np.float32).astype(dtype).astype(np.float64)
    return np.moveaxis((codes * scale).reshape(v.shape), -1, axis)


WIDE = False


def mx_kscale(k):
    if not WIDE:
        return np.ones(k)
    levels = np.array([10, -10, 5, -5, 0])
    a = np.random.permutation(np.resize(levels, k // 512 * 4)).reshape(k // 512, 4)
    idx = np.arange(k)
    return np.exp2(a[idx // 512, idx % 128 // 32])


BF16 = ml_dtypes.bfloat16


def bf(x):
    return np.asarray(x, np.float32).astype(BF16)


def f64(x):
    return np.asarray(x).astype(np.float64)


E2M1 = np.array([0.0, 0.5, 1.0, 1.5, 2.0, 3.0, 4.0, 6.0, -0.0, -0.5, -1.0, -1.5, -2.0, -3.0, -4.0, -6.0])


def pack_weight(w, fmt):
    k, n = w.shape
    w = f64(bf(w)).reshape(k // 32, 32, n)
    amax = np.abs(w).max(1)
    if fmt == "e4m3":
        byte = np.frexp(amax)[1] - 1 + 127 - 7
    else:
        mant, ex = np.frexp(amax / 6.0)
        byte = np.where(mant > 0.5, ex, ex - 1) + 127
    byte = np.clip(np.where(amax > 0, byte, 1), 1, 254)
    scaled = (w * np.exp2(127.0 - byte)[:, None, :]).reshape(k, n).astype(np.float32)
    by_word = np.ascontiguousarray(scaled.reshape(k // 512, 128, 4, n).transpose(0, 1, 3, 2))
    if fmt == "e4m3":
        words = by_word.astype(ml_dtypes.float8_e4m3fn).view(np.uint8)
    else:
        c = by_word.astype(ml_dtypes.float4_e2m1fn).view(np.uint8) & 0xF
        words = c[..., 0::2] | (c[..., 1::2] << 4)
    return np.ascontiguousarray(words), np.ascontiguousarray(byte.astype(np.uint8).reshape(k // 512, 16, n))


def unpack_weight(words, scales, fmt):
    g, p, n, _ = words.shape
    if fmt == "e4m3":
        vals = np.ascontiguousarray(words).view(ml_dtypes.float8_e4m3fn).astype(np.float64)
    else:
        nib = np.empty((g, p, n, 4), np.uint8)
        nib[..., 0::2] = words & 0xF
        nib[..., 1::2] = words >> 4
        vals = E2M1[nib]
    vals = vals * np.repeat(np.exp2(scales.astype(np.float64) - 127.0), 8, axis=1)[..., None]
    return vals.transpose(0, 1, 3, 2).reshape(g * 512, n)

def pack4(w):
    words, scales = pack_weight(w, "e2m1")
    return words.reshape(words.shape[0], 128, -1), scales


def unpack4(words, scales):
    return unpack_weight(words.reshape(words.shape[0], 128, -1, 2), scales, "e2m1")


B, GH, GW, F_IN, F_OUT = 2, 64, 64, 512, 512


def setup_inputs():
    s = mx_kscale(F_IN)
    X = bf(np.random.standard_normal((B, GH * GW, F_IN)) * s)
    words, scales = pack4(np.random.standard_normal((F_IN, F_OUT)) * 0.5 / np.sqrt(F_IN) / s[:, None])
    b = bf(np.random.standard_normal(F_OUT) * 0.3)
    return {"X": X,
            "W_gcn_words": words,
            "W_gcn_scales": scales,
            "b": b,
            "H": GH, "Wd": GW}


def _neighbor_sum(Xg):
    p = np.pad(Xg, ((0, 0), (1, 1), (1, 1), (0, 0)))
    return (p[:, :-2, 1:-1] + p[:, 2:, 1:-1]
            + p[:, 1:-1, :-2] + p[:, 1:-1, 2:])


def reference(X, W_gcn_words, W_gcn_scales, b, H, Wd):
    X = f64(X)
    Bn, N, F = X.shape
    Xg = X.reshape(Bn, H, Wd, F)
    AX = _neighbor_sum(Xg).reshape(Bn, N, F)
    return (mxq(AX, 2, "e4m3") @ unpack4(W_gcn_words, W_gcn_scales)) + f64(b)

@@ -1,0 +1,214 @@
+from contextlib import ExitStack
+
+import concourse.mybir as mybir
+from concourse.masks import make_identity
+
+F32 = mybir.dt.float32
+BF16 = mybir.dt.bfloat16
+U8 = mybir.dt.uint8
+U32 = mybir.dt.uint32
+I32 = mybir.dt.int32
+FP8X4 = mybir.dt.float8_e4m3fn_x4
+FP4X4 = mybir.dt.float4_e2m1fn_x4
+ADD = mybir.AluOpType.add
+MULT = mybir.AluOpType.mult
+
+P = 128
+PACK = 4
+BATCH = 2
+GRID = 64
+F_IN = 512
+F_OUT = 512
+PAIR = 2
+N_PAIRS = GRID // PAIR
+LOADED_AHEAD = 12
+WIDENED_AHEAD = 5
+
+FLOPS = 2 * BATCH * GRID * GRID * F_IN * F_OUT
+
+
+def tile_graphconvlayer_kernel(tc, X, W_gcn_words, W_gcn_scales, b, H, Wd, out):
+    nc = tc.nc
+    assert (H, Wd) == (GRID, GRID)
+    assert BATCH * GRID == P and PACK * P == F_IN
+
+    x_rows = X.rearrange("b (i j) f -> i j b f", j=GRID)
+    x_last_column = X.rearrange("b (i j) f -> j i b f", j=GRID)[GRID - 1]
+    out_rows = out.rearrange("b (i j) n -> i j b n", j=GRID)
+
+    with ExitStack() as ctx:
+        const = ctx.enter_context(tc.tile_pool(name="const", bufs=1))
+        raw_pool = ctx.enter_context(tc.tile_pool(name="raw", bufs=LOADED_AHEAD))
+        wide_pool = ctx.enter_context(tc.tile_pool(name="wide", bufs=8))
+        kept_pool = ctx.enter_context(tc.tile_pool(name="kept", bufs=6))
+        grouped_pool = ctx.enter_context(tc.tile_pool(name="grouped", bufs=3))
+        mx_pool = ctx.enter_context(tc.tile_pool(name="mx", bufs=3))
+        result_pool = ctx.enter_context(tc.tile_pool(name="result", bufs=6))
+        sums_psum = ctx.enter_context(tc.psum_pool(name="sums_psum", bufs=5))
+        prod_psum = ctx.enter_context(tc.psum_pool(name="prod_psum", bufs=3))
+        ctx.enter_context(tc.manual_schedule())
+
+        raw = {}
+        wide = {}
+        half = {}
+        kept = {}
+        grouped = {}
+        codes = {}
+        scales = {}
+        product = {}
+
+        def load_row(i):
+            x_raw = raw_pool.tile([P, F_IN], BF16)
+            nc.sync.dma_start(out=x_raw[:], in_=x_rows[i])
+            raw[i] = x_raw
+
+        def widen(engine_is_scalar, x_wide, x_raw):
+            dst = x_wide[:].rearrange("c t q -> c q t")
+            src = x_raw[:].rearrange("c (q t) -> c q t", t=PACK)
+            if engine_is_scalar:
+                nc.scalar.copy(out=dst, in_=src)
+            else:
+                nc.gpsimd.tensor_scalar(out=dst, in0=src, scalar1=1.0, scalar2=0.0, op0=MULT, op1=ADD)
+
+        def widen_row(i):
+            x_wide = wide_pool.tile([P, PACK, P], F32)
+            widen(i % 2 == 0, x_wide, raw[i])
+            wide[i] = x_wide
+
+        def half_sums(i):
+            acc = sums_psum.tile([P, PACK, P], F32, tag="acc")
+            for t in range(PACK):
+                if i < GRID:
+                    nc.tensor.matmul(
+                        out=acc[:, t, :],
+                        lhsT=wide[i][:, t, :],
+                        rhs=shift_right[:],
+                        is_transpose=True,
+                        start=True,
+                        stop=(i == 0),
+                    )
+                if i > 0:
+                    nc.tensor.matmul(
+                        out=acc[:, t, :],
+                        lhsT=wide[i - 1][:, t, :],
+                        rhs=ident[:],
+                        is_transpose=True,
+                        start=(i == GRID),
+                        stop=True,
+                    )
+            half[i] = acc
+
+        def keep_half_sums(i):
+            in_sbuf = kept_pool.tile([P, PACK, P + BATCH], F32)
+            nc.scalar.copy(out=in_sbuf[:, :, 0:P], in_=half[i][:])
+            nc.scalar.copy(out=in_sbuf[:, :, P : P + BATCH], in_=last_column[:, :, BATCH * i : BATCH * (i + 1)])
+            kept[i] = in_sbuf
+
+        def neighbour_sum(i):
+            if i % PAIR == 0:
+                ax = grouped_pool.tile([P, PAIR, P, PACK], BF16, align_bytes=64)
+                grouped[i // PAIR] = ax
+            dst = grouped[i // PAIR][:, i % PAIR, :, :]
+            right_and_below = kept[i + 1][:, :, BATCH : P + BATCH].rearrange("q t c -> q c t")
+            if i % 2 == 0:
+                above_and_left = half[i][:].rearrange("q t c -> q c t")
+                nc.vector.tensor_tensor(out=dst, in0=above_and_left, in1=right_and_below, op=ADD)
+            else:
+                above_and_left = kept[i][:, :, 0:P].rearrange("q t c -> q c t")
+                nc.gpsimd.tensor_tensor(out=dst, in0=above_and_left, in1=right_and_below, op=ADD)
+
+        def quantise(pair):
+            ax_codes = mx_pool.tile([P, PAIR * P], U32, align_bytes=64)
+            ax_scales = mx_pool.tile([P, PAIR * P], U8, align_bytes=64)
+            nc.vector.quantize_mx(
+                out=ax_codes[:].bitcast(FP8X4),
+                scales=ax_scales[:],
+                in_=grouped[pair][:].rearrange("q r c t -> q (r c t)"),
+            )
+            codes[pair] = ax_codes
+            scales[pair] = ax_scales
+
+        def multiply(i):
+            prod = prod_psum.tile([P, F_OUT], F32)
+            cols = slice((i % PAIR) * P, (i % PAIR + 1) * P)
+            nc.tensor.matmul_mx(
+                out=prod[:],
+                lhsT=codes[i // PAIR][:, cols].bitcast(FP8X4),
+                lhsT_scale=scales[i // PAIR][:, cols],
+                rhs=w_words[:].bitcast(FP4X4),
+                rhs_scale=w_scales[:],
+                start=True,
+                stop=True,
+            )
+            product[i] = prod
+
+        def add_bias_and_store(i):
+            result = result_pool.tile([P, F_OUT], F32)
+            nc.vector.tensor_tensor(out=result[:], in0=product[i][:], in1=bias[:], op=ADD)
+            nc.sync.dma_start(out=out_rows[i], in_=result[:])
+
+        ident = const.tile([P, P], F32)
+        make_identity(nc, ident[:])
+        shift_right = const.tile([P, P], F32)
+        nc.vector.memset(shift_right[:], 0.0)
+        nc.vector.tensor_copy(out=shift_right[:, BATCH:P], in_=ident[:, 0 : P - BATCH])
+        last_column = const.tile([P, PACK, P + BATCH], F32)
+        nc.vector.memset(last_column[:], 0.0)
+        w_scales = const.tile([P, F_OUT], U8, align_bytes=64)
+        nc.vector.memset(w_scales[:].bitcast(I32), 0)
+        w_words = const.tile([P, 2 * F_OUT], U8, align_bytes=64)
+        bias = const.tile([P, F_OUT], BF16)
+        nc.scalar.dma_start(out=bias[:], in_=b.partition_broadcast(P))
+
+        for i in range(3):
+            load_row(i)
+        edge_raw = const.tile([P, F_IN], BF16)
+        nc.sync.dma_start(out=edge_raw[:], in_=x_last_column)
+        for i in range(3, WIDENED_AHEAD):
+            load_row(i)
+        nc.sync.dma_start(out=w_words[:].bitcast(I32), in_=W_gcn_words[0].bitcast(I32))
+        for quadrant in range(4):
+            nc.sync.dma_start(
+                out=w_scales[32 * quadrant : 32 * quadrant + 4, :].bitcast(I32),
+                in_=W_gcn_scales[0, 4 * quadrant : 4 * quadrant + 4, :].bitcast(I32),
+            )
+        for i in range(WIDENED_AHEAD, LOADED_AHEAD):
+            load_row(i)
+
+        for i in range(3):
+            widen_row(i)
+        edge_wide = const.tile([P, PACK, P], F32)
+        widen(True, edge_wide, edge_raw)
+        for i in range(3, WIDENED_AHEAD):
+            widen_row(i)
+        half_sums(0)
+        edge_t = sums_psum.tile([P, PACK, P], F32, tag="acc")
+        for t in range(PACK):
+            nc.tensor.transpose(edge_t[:, t, :], edge_wide[:, t, :], ident[:])
+        nc.scalar.copy(out=last_column[:, :, 0:P], in_=edge_t[:])
+
+        for step in range(N_PAIRS + 2):
+            first = PAIR * step
+            if step < N_PAIRS:
+                half_sums(first + 1)
+                half_sums(first + 2)
+            if step >= 2:
+                multiply(first - 4)
+                multiply(first - 3)
+            if step < N_PAIRS:
+                keep_half_sums(first + 1)
+                keep_half_sums(first + 2)
+                neighbour_sum(first)
+                neighbour_sum(first + 1)
+            for i in (first + WIDENED_AHEAD, first + WIDENED_AHEAD + 1):
+                if i < GRID:
+                    widen_row(i)
+            if step >= 2:
+                add_bias_and_store(first - 4)
+            if 1 <= step <= N_PAIRS:
+                quantise(step - 1)
+            if step >= 2:
+                add_bias_and_store(first - 3)
+            for i in (first + LOADED_AHEAD, first + LOADED_AHEAD + 1):
+                if i < GRID:
+                    load_row(i)

@@ -72,7 +72,7 @@ def tile_graphconvlayer_kernel(tc, X, W_gcn_words, W_gcn_scales, b, H, Wd, out):
 
         def widen_row(i):
             x_wide = wide_pool.tile([P, PACK, P], F32)
-            widen(i % 2 == 0, x_wide, raw[i])
+            widen(True, x_wide, raw[i])
             wide[i] = x_wide
 
         def half_sums(i):
@@ -110,12 +110,8 @@ def tile_graphconvlayer_kernel(tc, X, W_gcn_words, W_gcn_scales, b, H, Wd, out):
                 grouped[i // PAIR] = ax
             dst = grouped[i // PAIR][:, i % PAIR, :, :]
             right_and_below = kept[i + 1][:, :, BATCH : P + BATCH].rearrange("q t c -> q c t")
-            if i % 2 == 0:
-                above_and_left = half[i][:].rearrange("q t c -> q c t")
-                nc.vector.tensor_tensor(out=dst, in0=above_and_left, in1=right_and_below, op=ADD)
-            else:
-                above_and_left = kept[i][:, :, 0:P].rearrange("q t c -> q c t")
-                nc.gpsimd.tensor_tensor(out=dst, in0=above_and_left, in1=right_and_below, op=ADD)
+            above_and_left = half[i][:].rearrange("q t c -> q c t")
+            nc.vector.tensor_tensor(out=dst, in0=above_and_left, in1=right_and_below, op=ADD)
 
         def quantise(pair):
             ax_codes = mx_pool.tile([P, PAIR * P], U32, align_bytes=64)

@@ -63,16 +63,23 @@ def tile_graphconvlayer_kernel(tc, X, W_gcn_words, W_gcn_scales, b, H, Wd, out):
             raw[i] = x_raw
 
         def widen(engine_is_scalar, x_wide, x_raw):
-            dst = x_wide[:].rearrange("c t q -> c q t")
-            src = x_raw[:].rearrange("c (q t) -> c q t", t=PACK)
             if engine_is_scalar:
-                nc.scalar.copy(out=dst, in_=src)
+                nc.scalar.copy(
+                    out=x_wide[:].rearrange("c t q -> c q t"), in_=x_raw[:].rearrange("c (q t) -> c q t", t=PACK)
+                )
             else:
-                nc.gpsimd.tensor_scalar(out=dst, in0=src, scalar1=1.0, scalar2=0.0, op0=MULT, op1=ADD)
+                nc.gpsimd.tensor_scalar(
+                    out=x_wide[:],
+                    in0=x_raw[:].rearrange("c (q t) -> c t q", t=PACK),
+                    scalar1=1.0,
+                    scalar2=0.0,
+                    op0=MULT,
+                    op1=ADD,
+                )
 
         def widen_row(i):
             x_wide = wide_pool.tile([P, PACK, P], F32)
-            widen(True, x_wide, raw[i])
+            widen(i % 2 == 0, x_wide, raw[i])
             wide[i] = x_wide
 
         def half_sums(i):
@@ -99,9 +106,9 @@ def tile_graphconvlayer_kernel(tc, X, W_gcn_words, W_gcn_scales, b, H, Wd, out):
             half[i] = acc
 
         def keep_half_sums(i):
-            in_sbuf = kept_pool.tile([P, PACK, P + BATCH], F32)
-            nc.scalar.copy(out=in_sbuf[:, :, 0:P], in_=half[i][:])
-            nc.scalar.copy(out=in_sbuf[:, :, P : P + BATCH], in_=last_column[:, :, BATCH * i : BATCH * (i + 1)])
+            in_sbuf = kept_pool.tile([P, P + BATCH, PACK], F32)
+            nc.scalar.copy(out=in_sbuf[:, 0:P, :], in_=half[i][:].rearrange("q t c -> q c t"))
+            nc.scalar.copy(out=in_sbuf[:, P : P + BATCH, :], in_=last_column[:, BATCH * i : BATCH * (i + 1), :])
             kept[i] = in_sbuf
 
         def neighbour_sum(i):
@@ -109,9 +116,13 @@ def tile_graphconvlayer_kernel(tc, X, W_gcn_words, W_gcn_scales, b, H, Wd, out):
                 ax = grouped_pool.tile([P, PAIR, P, PACK], BF16, align_bytes=64)
                 grouped[i // PAIR] = ax
             dst = grouped[i // PAIR][:, i % PAIR, :, :]
-            right_and_below = kept[i + 1][:, :, BATCH : P + BATCH].rearrange("q t c -> q c t")
-            above_and_left = half[i][:].rearrange("q t c -> q c t")
-            nc.vector.tensor_tensor(out=dst, in0=above_and_left, in1=right_and_below, op=ADD)
+            right_and_below = kept[i + 1][:, BATCH : P + BATCH, :]
+            if i % 2 == 0:
+                above_and_left = half[i][:].rearrange("q t c -> q c t")
+                nc.vector.tensor_tensor(out=dst, in0=above_and_left, in1=right_and_below, op=ADD)
+            else:
+                above_and_left = kept[i][:, 0:P, :]
+                nc.gpsimd.tensor_tensor(out=dst, in0=above_and_left, in1=right_and_below, op=ADD)
 
         def quantise(pair):
             ax_codes = mx_pool.tile([P, PAIR * P], U32, align_bytes=64)
@@ -148,7 +159,7 @@ def tile_graphconvlayer_kernel(tc, X, W_gcn_words, W_gcn_scales, b, H, Wd, out):
         shift_right = const.tile([P, P], F32)
         nc.vector.memset(shift_right[:], 0.0)
         nc.vector.tensor_copy(out=shift_right[:, BATCH:P], in_=ident[:, 0 : P - BATCH])
-        last_column = const.tile([P, PACK, P + BATCH], F32)
+        last_column = const.tile([P, P + BATCH, PACK], F32)
         nc.vector.memset(last_column[:], 0.0)
         w_scales = const.tile([P, F_OUT], U8, align_bytes=64)
         nc.vector.memset(w_scales[:].bitcast(I32), 0)
@@ -181,7 +192,7 @@ def tile_graphconvlayer_kernel(tc, X, W_gcn_words, W_gcn_scales, b, H, Wd, out):
         edge_t = sums_psum.tile([P, PACK, P], F32, tag="acc")
         for t in range(PACK):
             nc.tensor.transpose(edge_t[:, t, :], edge_wide[:, t, :], ident[:])
-        nc.scalar.copy(out=last_column[:, :, 0:P], in_=edge_t[:])
+        nc.scalar.copy(out=last_column[:, 0:P, :], in_=edge_t[:].rearrange("q t c -> q c t"))
 
         for step in range(N_PAIRS + 2):
             first = PAIR * step

@@ -82,28 +82,33 @@ def tile_graphconvlayer_kernel(tc, X, W_gcn_words, W_gcn_scales, b, H, Wd, out):
             widen(i % 2 == 0, x_wide, raw[i])
             wide[i] = x_wide
 
-        def half_sums(i):
+
+        def left_neighbours(i):
             acc = sums_psum.tile([P, PACK, P], F32, tag="acc")
             for t in range(PACK):
-                if i < GRID:
-                    nc.tensor.matmul(
-                        out=acc[:, t, :],
-                        lhsT=wide[i][:, t, :],
-                        rhs=shift_right[:],
-                        is_transpose=True,
-                        start=True,
-                        stop=(i == 0),
-                    )
-                if i > 0:
-                    nc.tensor.matmul(
-                        out=acc[:, t, :],
-                        lhsT=wide[i - 1][:, t, :],
-                        rhs=ident[:],
-                        is_transpose=True,
-                        start=(i == GRID),
-                        stop=True,
-                    )
+                nc.tensor.matmul(
+                    out=acc[:, t, :],
+                    lhsT=wide[i][:, t, :],
+                    rhs=shift_right[:],
+                    is_transpose=True,
+                    start=(t == 0),
+                    stop=(i == 0 and t == PACK - 1),
+                )
             half[i] = acc
+
+        def neighbours_above(i):
+            if i == GRID:
+                acc = sums_psum.tile([P, PACK, P], F32, tag="acc")
+                half[i] = acc
+            for t in range(PACK):
+                nc.tensor.matmul(
+                    out=half[i][:, t, :],
+                    lhsT=wide[i - 1][:, t, :],
+                    rhs=ident[:],
+                    is_transpose=True,
+                    start=(i == GRID and t == 0),
+                    stop=(t == PACK - 1),
+                )
 
         def keep_half_sums(i):
             in_sbuf = kept_pool.tile([P, P + BATCH, PACK], F32)
@@ -188,7 +193,7 @@ def tile_graphconvlayer_kernel(tc, X, W_gcn_words, W_gcn_scales, b, H, Wd, out):
         widen(True, edge_wide, edge_raw)
         for i in range(3, WIDENED_AHEAD):
             widen_row(i)
-        half_sums(0)
+        left_neighbours(0)
         edge_t = sums_psum.tile([P, PACK, P], F32, tag="acc")
         for t in range(PACK):
             nc.tensor.transpose(edge_t[:, t, :], edge_wide[:, t, :], ident[:])
@@ -197,8 +202,11 @@ def tile_graphconvlayer_kernel(tc, X, W_gcn_words, W_gcn_scales, b, H, Wd, out):
         for step in range(N_PAIRS + 2):
             first = PAIR * step
             if step < N_PAIRS:
-                half_sums(first + 1)
-                half_sums(first + 2)
+                left_neighbours(first + 1)
+                if first + 2 < GRID:
+                    left_neighbours(first + 2)
+                neighbours_above(first + 1)
+                neighbours_above(first + 2)
             if step >= 2:
                 multiply(first - 4)
                 multiply(first - 3)

@@ -11,7 +11,6 @@ I32 = mybir.dt.int32
 FP8X4 = mybir.dt.float8_e4m3fn_x4
 FP4X4 = mybir.dt.float4_e2m1fn_x4
 ADD = mybir.AluOpType.add
-MULT = mybir.AluOpType.mult
 
 P = 128
 PACK = 4
@@ -62,24 +61,14 @@ def tile_graphconvlayer_kernel(tc, X, W_gcn_words, W_gcn_scales, b, H, Wd, out):
             nc.sync.dma_start(out=x_raw[:], in_=x_rows[i])
             raw[i] = x_raw
 
-        def widen(engine_is_scalar, x_wide, x_raw):
-            if engine_is_scalar:
-                nc.scalar.copy(
-                    out=x_wide[:].rearrange("c t q -> c q t"), in_=x_raw[:].rearrange("c (q t) -> c q t", t=PACK)
-                )
-            else:
-                nc.gpsimd.tensor_scalar(
-                    out=x_wide[:],
-                    in0=x_raw[:].rearrange("c (q t) -> c t q", t=PACK),
-                    scalar1=1.0,
-                    scalar2=0.0,
-                    op0=MULT,
-                    op1=ADD,
-                )
+        def widen(x_wide, x_raw):
+            nc.scalar.copy(
+                out=x_wide[:].rearrange("c t q -> c q t"), in_=x_raw[:].rearrange("c (q t) -> c q t", t=PACK)
+            )
 
         def widen_row(i):
             x_wide = wide_pool.tile([P, PACK, P], F32)
-            widen(i % 2 == 0, x_wide, raw[i])
+            widen(x_wide, raw[i])
             wide[i] = x_wide
 
 
@@ -190,7 +179,7 @@ def tile_graphconvlayer_kernel(tc, X, W_gcn_words, W_gcn_scales, b, H, Wd, out):
         for i in range(3):
             widen_row(i)
         edge_wide = const.tile([P, PACK, P], F32)
-        widen(True, edge_wide, edge_raw)
+        widen(edge_wide, edge_raw)
         for i in range(3, WIDENED_AHEAD):
             widen_row(i)
         left_neighbours(0)

@@ -40,7 +40,7 @@ def tile_graphconvlayer_kernel(tc, X, W_gcn_words, W_gcn_scales, b, H, Wd, out):
         raw_pool = ctx.enter_context(tc.tile_pool(name="raw", bufs=LOADED_AHEAD))
         wide_pool = ctx.enter_context(tc.tile_pool(name="wide", bufs=8))
         kept_pool = ctx.enter_context(tc.tile_pool(name="kept", bufs=6))
-        grouped_pool = ctx.enter_context(tc.tile_pool(name="grouped", bufs=3))
+        grouped_pool = ctx.enter_context(tc.tile_pool(name="grouped", bufs=1))
         mx_pool = ctx.enter_context(tc.tile_pool(name="mx", bufs=3))
         result_pool = ctx.enter_context(tc.tile_pool(name="result", bufs=6))
         sums_psum = ctx.enter_context(tc.psum_pool(name="sums_psum", bufs=5))
@@ -199,6 +199,8 @@ def tile_graphconvlayer_kernel(tc, X, W_gcn_words, W_gcn_scales, b, H, Wd, out):
             if step >= 2:
                 multiply(first - 4)
                 multiply(first - 3)
+            if 1 <= step <= N_PAIRS:
+                quantise(step - 1)
             if step < N_PAIRS:
                 keep_half_sums(first + 1)
                 keep_half_sums(first + 2)
@@ -209,9 +211,6 @@ def tile_graphconvlayer_kernel(tc, X, W_gcn_words, W_gcn_scales, b, H, Wd, out):
                     widen_row(i)
             if step >= 2:
                 add_bias_and_store(first - 4)
-            if 1 <= step <= N_PAIRS:
-                quantise(step - 1)
-            if step >= 2:
                 add_bias_and_store(first - 3)
             for i in (first + LOADED_AHEAD, first + LOADED_AHEAD + 1):
                 if i < GRID:

@@ -22,6 +22,7 @@ PAIR = 2
 N_PAIRS = GRID // PAIR
 LOADED_AHEAD = 12
 WIDENED_AHEAD = 5
+QUANTISE_LAG = 2
 
 FLOPS = 2 * BATCH * GRID * GRID * F_IN * F_OUT
 
@@ -39,8 +40,7 @@ def tile_graphconvlayer_kernel(tc, X, W_gcn_words, W_gcn_scales, b, H, Wd, out):
         const = ctx.enter_context(tc.tile_pool(name="const", bufs=1))
         raw_pool = ctx.enter_context(tc.tile_pool(name="raw", bufs=LOADED_AHEAD))
         wide_pool = ctx.enter_context(tc.tile_pool(name="wide", bufs=8))
-        kept_pool = ctx.enter_context(tc.tile_pool(name="kept", bufs=6))
-        grouped_pool = ctx.enter_context(tc.tile_pool(name="grouped", bufs=1))
+        grouped_pool = ctx.enter_context(tc.tile_pool(name="grouped", bufs=QUANTISE_LAG))
         mx_pool = ctx.enter_context(tc.tile_pool(name="mx", bufs=3))
         result_pool = ctx.enter_context(tc.tile_pool(name="result", bufs=6))
         sums_psum = ctx.enter_context(tc.psum_pool(name="sums_psum", bufs=5))
@@ -100,9 +100,8 @@ def tile_graphconvlayer_kernel(tc, X, W_gcn_words, W_gcn_scales, b, H, Wd, out):
                 )
 
         def keep_half_sums(i):
-            in_sbuf = kept_pool.tile([P, P + BATCH, PACK], F32)
+            in_sbuf = kept_all[:, i - 1, :, :]
             nc.scalar.copy(out=in_sbuf[:, 0:P, :], in_=half[i][:].rearrange("q t c -> q c t"))
-            nc.scalar.copy(out=in_sbuf[:, P : P + BATCH, :], in_=last_column[:, BATCH * i : BATCH * (i + 1), :])
             kept[i] = in_sbuf
 
         def neighbour_sum(i):
@@ -153,6 +152,7 @@ def tile_graphconvlayer_kernel(tc, X, W_gcn_words, W_gcn_scales, b, H, Wd, out):
         shift_right = const.tile([P, P], F32)
         nc.vector.memset(shift_right[:], 0.0)
         nc.vector.tensor_copy(out=shift_right[:, BATCH:P], in_=ident[:, 0 : P - BATCH])
+        kept_all = const.tile([P, GRID, P + BATCH, PACK], F32)
         last_column = const.tile([P, P + BATCH, PACK], F32)
         nc.vector.memset(last_column[:], 0.0)
         w_scales = const.tile([P, F_OUT], U8, align_bytes=64)
@@ -187,31 +187,36 @@ def tile_graphconvlayer_kernel(tc, X, W_gcn_words, W_gcn_scales, b, H, Wd, out):
         for t in range(PACK):
             nc.tensor.transpose(edge_t[:, t, :], edge_wide[:, t, :], ident[:])
         nc.scalar.copy(out=last_column[:, 0:P, :], in_=edge_t[:].rearrange("q t c -> q c t"))
+        nc.vector.tensor_copy(
+            out=kept_all[:, :, P : P + BATCH, :],
+            in_=last_column[:, BATCH : P + BATCH, :].rearrange("q (i b) t -> q i b t", b=BATCH),
+        )
 
-        for step in range(N_PAIRS + 2):
+        for step in range(N_PAIRS + QUANTISE_LAG + 1):
             first = PAIR * step
+            done = first - PAIR * (QUANTISE_LAG + 1)
             if step < N_PAIRS:
                 left_neighbours(first + 1)
                 if first + 2 < GRID:
                     left_neighbours(first + 2)
                 neighbours_above(first + 1)
                 neighbours_above(first + 2)
-            if step >= 2:
-                multiply(first - 4)
-                multiply(first - 3)
-            if 1 <= step <= N_PAIRS:
-                quantise(step - 1)
+            if done >= 0:
+                multiply(done)
+                multiply(done + 1)
+            if 0 <= step - QUANTISE_LAG < N_PAIRS:
+                quantise(step - QUANTISE_LAG)
             if step < N_PAIRS:
                 keep_half_sums(first + 1)
                 keep_half_sums(first + 2)
                 neighbour_sum(first)
                 neighbour_sum(first + 1)
+            if done >= 0:
+                add_bias_and_store(done)
+                add_bias_and_store(done + 1)
             for i in (first + WIDENED_AHEAD, first + WIDENED_AHEAD + 1):
                 if i < GRID:
                     widen_row(i)
-            if step >= 2:
-                add_bias_and_store(first - 4)
-                add_bias_and_store(first - 3)
             for i in (first + LOADED_AHEAD, first + LOADED_AHEAD + 1):
                 if i < GRID:
                     load_row(i)

@@ -22,7 +22,8 @@ PAIR = 2
 N_PAIRS = GRID // PAIR
 LOADED_AHEAD = 12
 WIDENED_AHEAD = 5
-QUANTISE_LAG = 2
+VECTOR_KEEPS_EVERY = 0
+QUANTISE_LAG = 1
 
 FLOPS = 2 * BATCH * GRID * GRID * F_IN * F_OUT
 
@@ -66,41 +67,46 @@ def tile_graphconvlayer_kernel(tc, X, W_gcn_words, W_gcn_scales, b, H, Wd, out):
                 out=x_wide[:].rearrange("c t q -> c q t"), in_=x_raw[:].rearrange("c (q t) -> c q t", t=PACK)
             )
 
+        def widen_on_vector(x_wide, x_raw):
+            nc.vector.tensor_copy(out=x_wide[:], in_=x_raw[:].rearrange("c (q t) -> c t q", t=PACK))
+
+        def widen_row_on_vector(i):
+            x_wide = wide_pool.tile([P, PACK, P], F32)
+            widen_on_vector(x_wide, raw[i])
+            wide[i] = x_wide
+
         def widen_row(i):
             x_wide = wide_pool.tile([P, PACK, P], F32)
             widen(x_wide, raw[i])
             wide[i] = x_wide
 
 
-        def left_neighbours(i):
+        def transpose_row(r):
             acc = sums_psum.tile([P, PACK, P], F32, tag="acc")
+            half[r] = acc
+            if r == 0:
+                above = sums_psum.tile([P, PACK, P], F32, tag="acc")
+                half[-1] = above
             for t in range(PACK):
                 nc.tensor.matmul(
-                    out=acc[:, t, :],
-                    lhsT=wide[i][:, t, :],
+                    out=half[r][:, t, :],
+                    lhsT=wide[r][:, t, :],
                     rhs=shift_right[:],
                     is_transpose=True,
                     start=(t == 0),
-                    stop=(i == 0 and t == PACK - 1),
+                    stop=(r == GRID - 1 and t == PACK - 1),
                 )
-            half[i] = acc
-
-        def neighbours_above(i):
-            if i == GRID:
-                acc = sums_psum.tile([P, PACK, P], F32, tag="acc")
-                half[i] = acc
-            for t in range(PACK):
                 nc.tensor.matmul(
-                    out=half[i][:, t, :],
-                    lhsT=wide[i - 1][:, t, :],
+                    out=half[r - 1][:, t, :],
+                    lhsT=wide[r][:, t, :],
                     rhs=ident[:],
                     is_transpose=True,
-                    start=(i == GRID and t == 0),
+                    start=(r == 0 and t == 0),
                     stop=(t == PACK - 1),
                 )
 
         def keep_half_sums(i):
-            in_sbuf = kept_all[:, i - 1, :, :]
+            in_sbuf = kept_all[:, i + 1, :, :]
             nc.scalar.copy(out=in_sbuf[:, 0:P, :], in_=half[i][:].rearrange("q t c -> q c t"))
             kept[i] = in_sbuf
 
@@ -109,13 +115,13 @@ def tile_graphconvlayer_kernel(tc, X, W_gcn_words, W_gcn_scales, b, H, Wd, out):
                 ax = grouped_pool.tile([P, PAIR, P, PACK], BF16, align_bytes=64)
                 grouped[i // PAIR] = ax
             dst = grouped[i // PAIR][:, i % PAIR, :, :]
-            right_and_below = kept[i + 1][:, BATCH : P + BATCH, :]
-            if i % 2 == 0:
-                above_and_left = half[i][:].rearrange("q t c -> q c t")
-                nc.vector.tensor_tensor(out=dst, in0=above_and_left, in1=right_and_below, op=ADD)
+            right_and_above = kept[i - 1][:, BATCH : P + BATCH, :]
+            if i % 2 == 0 or i == GRID - 1:
+                left_and_below = half[i][:].rearrange("q t c -> q c t")
+                nc.vector.tensor_tensor(out=dst, in0=left_and_below, in1=right_and_above, op=ADD)
             else:
-                above_and_left = kept[i][:, 0:P, :]
-                nc.gpsimd.tensor_tensor(out=dst, in0=above_and_left, in1=right_and_below, op=ADD)
+                left_and_below = kept[i][:, 0:P, :]
+                nc.gpsimd.tensor_tensor(out=dst, in0=left_and_below, in1=right_and_above, op=ADD)
 
         def quantise(pair):
             ax_codes = mx_pool.tile([P, PAIR * P], U32, align_bytes=64)
@@ -176,39 +182,41 @@ def tile_graphconvlayer_kernel(tc, X, W_gcn_words, W_gcn_scales, b, H, Wd, out):
         for i in range(WIDENED_AHEAD, LOADED_AHEAD):
             load_row(i)
 
-        for i in range(3):
-            widen_row(i)
         edge_wide = const.tile([P, PACK, P], F32)
-        widen(edge_wide, edge_raw)
-        for i in range(3, WIDENED_AHEAD):
-            widen_row(i)
-        left_neighbours(0)
+        for i in range(WIDENED_AHEAD):
+            if i % 2 == 0:
+                widen_row(i)
+            else:
+                widen_row_on_vector(i)
+            if i == 1:
+                widen_on_vector(edge_wide, edge_raw)
+        transpose_row(0)
         edge_t = sums_psum.tile([P, PACK, P], F32, tag="acc")
         for t in range(PACK):
             nc.tensor.transpose(edge_t[:, t, :], edge_wide[:, t, :], ident[:])
-        nc.scalar.copy(out=last_column[:, 0:P, :], in_=edge_t[:].rearrange("q t c -> q c t"))
+        nc.vector.tensor_copy(out=last_column[:, BATCH : P + BATCH, :], in_=edge_t[:].rearrange("q t c -> q c t"))
         nc.vector.tensor_copy(
             out=kept_all[:, :, P : P + BATCH, :],
-            in_=last_column[:, BATCH : P + BATCH, :].rearrange("q (i b) t -> q i b t", b=BATCH),
+            in_=last_column[:, 0:P, :].rearrange("q (i b) t -> q i b t", b=BATCH),
         )
+        keep_half_sums(-1)
 
         for step in range(N_PAIRS + QUANTISE_LAG + 1):
             first = PAIR * step
             done = first - PAIR * (QUANTISE_LAG + 1)
             if step < N_PAIRS:
-                left_neighbours(first + 1)
+                transpose_row(first + 1)
                 if first + 2 < GRID:
-                    left_neighbours(first + 2)
-                neighbours_above(first + 1)
-                neighbours_above(first + 2)
+                    transpose_row(first + 2)
             if done >= 0:
                 multiply(done)
                 multiply(done + 1)
             if 0 <= step - QUANTISE_LAG < N_PAIRS:
                 quantise(step - QUANTISE_LAG)
             if step < N_PAIRS:
-                keep_half_sums(first + 1)
-                keep_half_sums(first + 2)
+                keep_half_sums(first)
+                if first + 1 < GRID - 1:
+                    keep_half_sums(first + 1)
                 neighbour_sum(first)
                 neighbour_sum(first + 1)
             if done >= 0:

@@ -20,8 +20,9 @@ F_IN = 512
 F_OUT = 512
 PAIR = 2
 N_PAIRS = GRID // PAIR
-LOADED_AHEAD = 12
-WIDENED_AHEAD = 5
+LOADED_AHEAD = 16
+WIDENED_AHEAD = 9
+SCALAR_WIDENS_FIRST = (0, 2, 4)
 VECTOR_KEEPS_EVERY = 0
 QUANTISE_LAG = 1
 
@@ -40,7 +41,7 @@ def tile_graphconvlayer_kernel(tc, X, W_gcn_words, W_gcn_scales, b, H, Wd, out):
     with ExitStack() as ctx:
         const = ctx.enter_context(tc.tile_pool(name="const", bufs=1))
         raw_pool = ctx.enter_context(tc.tile_pool(name="raw", bufs=LOADED_AHEAD))
-        wide_pool = ctx.enter_context(tc.tile_pool(name="wide", bufs=8))
+        wide_pool = ctx.enter_context(tc.tile_pool(name="wide", bufs=WIDENED_AHEAD + 3))
         grouped_pool = ctx.enter_context(tc.tile_pool(name="grouped", bufs=QUANTISE_LAG))
         mx_pool = ctx.enter_context(tc.tile_pool(name="mx", bufs=3))
         result_pool = ctx.enter_context(tc.tile_pool(name="result", bufs=6))
@@ -184,7 +185,7 @@ def tile_graphconvlayer_kernel(tc, X, W_gcn_words, W_gcn_scales, b, H, Wd, out):
 
         edge_wide = const.tile([P, PACK, P], F32)
         for i in range(WIDENED_AHEAD):
-            if i % 2 == 0:
+            if i in SCALAR_WIDENS_FIRST:
                 widen_row(i)
             else:
                 widen_row_on_vector(i)

@@ -166,7 +166,6 @@ def tile_graphconvlayer_kernel(tc, X, W_gcn_words, W_gcn_scales, b, H, Wd, out):
         nc.vector.memset(w_scales[:].bitcast(I32), 0)
         w_words = const.tile([P, 2 * F_OUT], U8, align_bytes=64)
         bias = const.tile([P, F_OUT], BF16)
-        nc.scalar.dma_start(out=bias[:], in_=b.partition_broadcast(P))
 
         for i in range(3):
             load_row(i)
@@ -191,6 +190,7 @@ def tile_graphconvlayer_kernel(tc, X, W_gcn_words, W_gcn_scales, b, H, Wd, out):
                 widen_row_on_vector(i)
             if i == 1:
                 widen_on_vector(edge_wide, edge_raw)
+        nc.scalar.dma_start(out=bias[:], in_=b.partition_broadcast(P))
         transpose_row(0)
         edge_t = sums_psum.tile([P, PACK, P], F32, tag="acc")
         for t in range(PACK):

@@ -18,13 +18,23 @@ BATCH = 2
 GRID = 64
 F_IN = 512
 F_OUT = 512
+
+T_ROWS = 40
 PAIR = 2
-N_PAIRS = GRID // PAIR
+N_PAIRS = T_ROWS // PAIR
 LOADED_AHEAD = 16
 WIDENED_AHEAD = 9
 SCALAR_WIDENS_FIRST = (0, 2, 4)
-VECTOR_KEEPS_EVERY = 0
-QUANTISE_LAG = 1
+
+BAND_ROWS = 6
+WIN_ROWS = 8
+WIN_COLS = 16
+WIN_STEP = 12
+WIN_EDGES = (0, 14, 26, 38, 50, 64)
+UNITS = ((0, 1, 2), (3, 4))
+BANDS = tuple((b, r0) for r0 in range(T_ROWS, GRID, BAND_ROWS) for b in range(BATCH))
+N_UNITS = len(BANDS) * len(UNITS)
+BAND_TILES = BAND_ROWS * GRID // P
 
 FLOPS = 2 * BATCH * GRID * GRID * F_IN * F_OUT
 
@@ -35,16 +45,19 @@ def tile_graphconvlayer_kernel(tc, X, W_gcn_words, W_gcn_scales, b, H, Wd, out):
     assert BATCH * GRID == P and PACK * P == F_IN
 
     x_rows = X.rearrange("b (i j) f -> i j b f", j=GRID)
+    x_cols = X.rearrange("b (i j) f -> b j i f", j=GRID)
     x_last_column = X.rearrange("b (i j) f -> j i b f", j=GRID)[GRID - 1]
     out_rows = out.rearrange("b (i j) n -> i j b n", j=GRID)
 
     with ExitStack() as ctx:
         const = ctx.enter_context(tc.tile_pool(name="const", bufs=1))
         raw_pool = ctx.enter_context(tc.tile_pool(name="raw", bufs=LOADED_AHEAD))
+        window_pool = ctx.enter_context(tc.tile_pool(name="window", bufs=13))
         wide_pool = ctx.enter_context(tc.tile_pool(name="wide", bufs=WIDENED_AHEAD + 3))
-        grouped_pool = ctx.enter_context(tc.tile_pool(name="grouped", bufs=QUANTISE_LAG))
+        grouped_pool = ctx.enter_context(tc.tile_pool(name="grouped", bufs=1))
+        band_pool = ctx.enter_context(tc.tile_pool(name="band", bufs=2))
         mx_pool = ctx.enter_context(tc.tile_pool(name="mx", bufs=3))
-        result_pool = ctx.enter_context(tc.tile_pool(name="result", bufs=6))
+        result_pool = ctx.enter_context(tc.tile_pool(name="result", bufs=8))
         sums_psum = ctx.enter_context(tc.psum_pool(name="sums_psum", bufs=5))
         prod_psum = ctx.enter_context(tc.psum_pool(name="prod_psum", bufs=3))
         ctx.enter_context(tc.manual_schedule())
@@ -57,46 +70,43 @@ def tile_graphconvlayer_kernel(tc, X, W_gcn_words, W_gcn_scales, b, H, Wd, out):
         codes = {}
         scales = {}
         product = {}
+        windows = {}
+        band_ax = {}
 
         def load_row(i):
             x_raw = raw_pool.tile([P, F_IN], BF16)
             nc.sync.dma_start(out=x_raw[:], in_=x_rows[i])
             raw[i] = x_raw
 
-        def widen(x_wide, x_raw):
-            nc.scalar.copy(
-                out=x_wide[:].rearrange("c t q -> c q t"), in_=x_raw[:].rearrange("c (q t) -> c q t", t=PACK)
-            )
-
-        def widen_on_vector(x_wide, x_raw):
-            nc.vector.tensor_copy(out=x_wide[:], in_=x_raw[:].rearrange("c (q t) -> c t q", t=PACK))
-
         def widen_row_on_vector(i):
             x_wide = wide_pool.tile([P, PACK, P], F32)
-            widen_on_vector(x_wide, raw[i])
+            nc.vector.tensor_copy(out=x_wide[:], in_=raw[i][:].rearrange("c (q t) -> c t q", t=PACK))
             wide[i] = x_wide
 
         def widen_row(i):
             x_wide = wide_pool.tile([P, PACK, P], F32)
-            widen(x_wide, raw[i])
+            nc.scalar.copy(
+                out=x_wide[:].rearrange("c t q -> c q t"), in_=raw[i][:].rearrange("c (q t) -> c q t", t=PACK)
+            )
             wide[i] = x_wide
 
-
         def transpose_row(r):
-            acc = sums_psum.tile([P, PACK, P], F32, tag="acc")
-            half[r] = acc
+            if r < T_ROWS:
+                acc = sums_psum.tile([P, PACK, P], F32, tag="acc")
+                half[r] = acc
             if r == 0:
                 above = sums_psum.tile([P, PACK, P], F32, tag="acc")
                 half[-1] = above
             for t in range(PACK):
-                nc.tensor.matmul(
-                    out=half[r][:, t, :],
-                    lhsT=wide[r][:, t, :],
-                    rhs=shift_right[:],
-                    is_transpose=True,
-                    start=(t == 0),
-                    stop=(r == GRID - 1 and t == PACK - 1),
-                )
+                if r < T_ROWS:
+                    nc.tensor.matmul(
+                        out=half[r][:, t, :],
+                        lhsT=wide[r][:, t, :],
+                        rhs=shift_right[:],
+                        is_transpose=True,
+                        start=(t == 0),
+                        stop=False,
+                    )
                 nc.tensor.matmul(
                     out=half[r - 1][:, t, :],
                     lhsT=wide[r][:, t, :],
@@ -117,7 +127,7 @@ def tile_graphconvlayer_kernel(tc, X, W_gcn_words, W_gcn_scales, b, H, Wd, out):
                 grouped[i // PAIR] = ax
             dst = grouped[i // PAIR][:, i % PAIR, :, :]
             right_and_above = kept[i - 1][:, BATCH : P + BATCH, :]
-            if i % 2 == 0 or i == GRID - 1:
+            if i % 2 == 0 or i == T_ROWS - 1:
                 left_and_below = half[i][:].rearrange("q t c -> q c t")
                 nc.vector.tensor_tensor(out=dst, in0=left_and_below, in1=right_and_above, op=ADD)
             else:
@@ -135,31 +145,115 @@ def tile_graphconvlayer_kernel(tc, X, W_gcn_words, W_gcn_scales, b, H, Wd, out):
             codes[pair] = ax_codes
             scales[pair] = ax_scales
 
-        def multiply(i):
+        def multiply(key, x_codes, x_scales, cols):
             prod = prod_psum.tile([P, F_OUT], F32)
-            cols = slice((i % PAIR) * P, (i % PAIR + 1) * P)
             nc.tensor.matmul_mx(
                 out=prod[:],
-                lhsT=codes[i // PAIR][:, cols].bitcast(FP8X4),
-                lhsT_scale=scales[i // PAIR][:, cols],
+                lhsT=x_codes[:, cols].bitcast(FP8X4),
+                lhsT_scale=x_scales[:, cols],
                 rhs=w_words[:].bitcast(FP4X4),
                 rhs_scale=w_scales[:],
                 start=True,
                 stop=True,
             )
-            product[i] = prod
+            product[key] = prod
 
-        def add_bias_and_store(i):
+        def multiply_row(i):
+            cols = slice((i % PAIR) * P, (i % PAIR + 1) * P)
+            multiply(i, codes[i // PAIR], scales[i // PAIR], cols)
+
+        def add_bias_and_store(key, dst):
             result = result_pool.tile([P, F_OUT], F32)
-            nc.vector.tensor_tensor(out=result[:], in0=product[i][:], in1=bias[:], op=ADD)
-            nc.sync.dma_start(out=out_rows[i], in_=result[:])
+            nc.vector.tensor_tensor(out=result[:], in0=product[key][:], in1=bias[:], op=ADD)
+            nc.sync.dma_start(out=dst, in_=result[:])
+
+        def load_unit(u):
+            batch, r0 = BANDS[u // len(UNITS)]
+            first_row = min(r0 - 1, GRID - WIN_ROWS)
+            for w in UNITS[u % len(UNITS)]:
+                x_win = window_pool.tile([P, F_IN], BF16)
+                nc.sync.dma_start(
+                    out=x_win[:],
+                    in_=x_cols[batch, WIN_STEP * w : WIN_STEP * w + WIN_COLS, first_row : first_row + WIN_ROWS, :],
+                )
+                windows[u, w] = x_win
+
+        def gather_unit(u):
+            batch, r0 = BANDS[u // len(UNITS)]
+            adjacency = adjacency_last if r0 + BAND_ROWS == GRID else adjacency_mid
+            unit = UNITS[u % len(UNITS)]
+            j0 = WIN_EDGES[unit[0]]
+            acc = sums_psum.tile([P, PACK, 256], BF16, tag="acc")
+            for w in unit:
+                j, end = WIN_EDGES[w], WIN_EDGES[w + 1]
+                c = j - WIN_STEP * w
+                for t in range(PACK):
+                    nc.tensor.matmul(
+                        out=acc[:, t, BAND_ROWS * (j - j0) : BAND_ROWS * (end - j0)],
+                        lhsT=windows[u, w][:].rearrange("p (q t) -> p t q", t=PACK)[:, t, :],
+                        rhs=adjacency[:, BAND_ROWS * c : BAND_ROWS * (c + end - j)],
+                        start=True,
+                        stop=True,
+                    )
+            return acc
+
+        def group_unit(u, acc):
+            band = u // len(UNITS)
+            unit = UNITS[u % len(UNITS)]
+            j, end = WIN_EDGES[unit[0]], WIN_EDGES[unit[-1] + 1]
+            if u % len(UNITS) == 0:
+                ax_band = band_pool.tile([P, BAND_ROWS, GRID, PACK], BF16, align_bytes=64)
+                band_ax[band] = ax_band
+            nc.scalar.copy(
+                out=band_ax[band][:, :, j:end, :],
+                in_=acc[:, :, 0 : BAND_ROWS * (end - j)].rearrange("q t (j r) -> q r j t", r=BAND_ROWS),
+            )
+
+        def quantise_band(band):
+            band_codes = mx_pool.tile([P, BAND_TILES * P], U32, align_bytes=64)
+            band_scales = mx_pool.tile([P, BAND_TILES * P], U8, align_bytes=64)
+            flat = band_ax[band][:].rearrange("q r j t -> q (r j t)")
+            for lo, hi in ((0, 2 * P), (2 * P, 3 * P)):
+                nc.vector.quantize_mx(
+                    out=band_codes[:, lo:hi].bitcast(FP8X4),
+                    scales=band_scales[:, lo:hi],
+                    in_=flat[:, PACK * lo : PACK * hi],
+                )
+            codes["band", band] = band_codes
+            scales["band", band] = band_scales
+
+        def multiply_band_tile(band, k):
+            multiply(("band", band, k), codes["band", band], scales["band", band], slice(k * P, (k + 1) * P))
+
+        def store_band_tile(band, k):
+            batch, r0 = BANDS[band]
+            node = (r0 + 2 * k) * GRID
+            add_bias_and_store(("band", band, k), out[batch, node : node + P, :])
 
         ident = const.tile([P, P], F32)
         make_identity(nc, ident[:])
         shift_right = const.tile([P, P], F32)
         nc.vector.memset(shift_right[:], 0.0)
         nc.vector.tensor_copy(out=shift_right[:, BATCH:P], in_=ident[:, 0 : P - BATCH])
-        kept_all = const.tile([P, GRID, P + BATCH, PACK], F32)
+        by_node = ident[:].rearrange("p (c r) -> p c r", r=WIN_ROWS)
+        adjacency_mid = const.tile([P, WIN_COLS * BAND_ROWS], BF16)
+        adjacency_last = const.tile([P, WIN_COLS * BAND_ROWS], BF16)
+
+        def build_adjacency(adjacency, r0):
+            a = adjacency[:].rearrange("p (c r) -> p c r", r=BAND_ROWS)
+            nc.vector.tensor_copy(out=a, in_=by_node[:, :, r0 - 1 : r0 - 1 + BAND_ROWS])
+            below = min(BAND_ROWS, WIN_ROWS - 1 - r0)
+            here = slice(r0, r0 + BAND_ROWS)
+            for out_part, in_part in (
+                (a[:, :, 0:below], by_node[:, :, r0 + 1 : r0 + 1 + below]),
+                (a[:, 1:WIN_COLS, :], by_node[:, 0 : WIN_COLS - 1, here]),
+                (a[:, 0 : WIN_COLS - 1, :], by_node[:, 1:WIN_COLS, here]),
+            ):
+                nc.vector.tensor_tensor(out=out_part, in0=out_part, in1=in_part, op=ADD)
+
+        build_adjacency(adjacency_mid, 1)
+        build_adjacency(adjacency_last, 2)
+        kept_all = const.tile([P, T_ROWS, P + BATCH, PACK], F32)
         last_column = const.tile([P, P + BATCH, PACK], F32)
         nc.vector.memset(last_column[:], 0.0)
         w_scales = const.tile([P, F_OUT], U8, align_bytes=64)
@@ -167,11 +261,20 @@ def tile_graphconvlayer_kernel(tc, X, W_gcn_words, W_gcn_scales, b, H, Wd, out):
         w_words = const.tile([P, 2 * F_OUT], U8, align_bytes=64)
         bias = const.tile([P, F_OUT], BF16)
 
+        units_of_step = {}
+        for u in range(N_UNITS):
+            units_of_step.setdefault(u * N_PAIRS // N_UNITS, []).append(u)
+        band_done_at = {band: (2 * band + 1) * N_PAIRS // N_UNITS for band in range(len(BANDS))}
+        UNITS_AHEAD = 4
+
         for i in range(3):
             load_row(i)
         edge_raw = const.tile([P, F_IN], BF16)
         nc.sync.dma_start(out=edge_raw[:], in_=x_last_column)
-        for i in range(3, WIDENED_AHEAD):
+        for i in range(3, 5):
+            load_row(i)
+        load_unit(0)
+        for i in range(5, WIDENED_AHEAD):
             load_row(i)
         nc.sync.dma_start(out=w_words[:].bitcast(I32), in_=W_gcn_words[0].bitcast(I32))
         for quadrant in range(4):
@@ -179,6 +282,8 @@ def tile_graphconvlayer_kernel(tc, X, W_gcn_words, W_gcn_scales, b, H, Wd, out):
                 out=w_scales[32 * quadrant : 32 * quadrant + 4, :].bitcast(I32),
                 in_=W_gcn_scales[0, 4 * quadrant : 4 * quadrant + 4, :].bitcast(I32),
             )
+        for u in range(1, UNITS_AHEAD):
+            load_unit(u)
         for i in range(WIDENED_AHEAD, LOADED_AHEAD):
             load_row(i)
 
@@ -189,7 +294,7 @@ def tile_graphconvlayer_kernel(tc, X, W_gcn_words, W_gcn_scales, b, H, Wd, out):
             else:
                 widen_row_on_vector(i)
             if i == 1:
-                widen_on_vector(edge_wide, edge_raw)
+                nc.vector.tensor_copy(out=edge_wide[:], in_=edge_raw[:].rearrange("c (q t) -> c t q", t=PACK))
         nc.scalar.dma_start(out=bias[:], in_=b.partition_broadcast(P))
         transpose_row(0)
         edge_t = sums_psum.tile([P, PACK, P], F32, tag="acc")
@@ -198,34 +303,48 @@ def tile_graphconvlayer_kernel(tc, X, W_gcn_words, W_gcn_scales, b, H, Wd, out):
         nc.vector.tensor_copy(out=last_column[:, BATCH : P + BATCH, :], in_=edge_t[:].rearrange("q t c -> q c t"))
         nc.vector.tensor_copy(
             out=kept_all[:, :, P : P + BATCH, :],
-            in_=last_column[:, 0:P, :].rearrange("q (i b) t -> q i b t", b=BATCH),
+            in_=last_column[:, 0 : BATCH * T_ROWS, :].rearrange("q (i b) t -> q i b t", b=BATCH),
         )
         keep_half_sums(-1)
 
-        for step in range(N_PAIRS + QUANTISE_LAG + 1):
+        for step in range(N_PAIRS + 2):
             first = PAIR * step
-            done = first - PAIR * (QUANTISE_LAG + 1)
+            done = first - 2 * PAIR
+            band_tiles = [(band, k) for band, at in band_done_at.items() for k in range(BAND_TILES) if at + 2 + k // 2 == step]
             if step < N_PAIRS:
                 transpose_row(first + 1)
-                if first + 2 < GRID:
-                    transpose_row(first + 2)
+                transpose_row(first + 2)
+            accs = [(u, gather_unit(u)) for u in units_of_step.get(step, [])]
             if done >= 0:
-                multiply(done)
-                multiply(done + 1)
-            if 0 <= step - QUANTISE_LAG < N_PAIRS:
-                quantise(step - QUANTISE_LAG)
+                multiply_row(done)
+                multiply_row(done + 1)
+            for band, k in band_tiles:
+                multiply_band_tile(band, k)
+            for band, at in band_done_at.items():
+                if at + 1 == step:
+                    quantise_band(band)
+            if 0 <= step - 1 < N_PAIRS:
+                quantise(step - 1)
             if step < N_PAIRS:
                 keep_half_sums(first)
-                if first + 1 < GRID - 1:
+                if first + 1 < T_ROWS - 1:
                     keep_half_sums(first + 1)
+            for u, acc in accs:
+                group_unit(u, acc)
+            if step < N_PAIRS:
                 neighbour_sum(first)
                 neighbour_sum(first + 1)
             if done >= 0:
-                add_bias_and_store(done)
-                add_bias_and_store(done + 1)
+                add_bias_and_store(done, out_rows[done])
+                add_bias_and_store(done + 1, out_rows[done + 1])
+            for band, k in band_tiles:
+                store_band_tile(band, k)
             for i in (first + WIDENED_AHEAD, first + WIDENED_AHEAD + 1):
-                if i < GRID:
+                if i <= T_ROWS:
                     widen_row(i)
             for i in (first + LOADED_AHEAD, first + LOADED_AHEAD + 1):
-                if i < GRID:
+                if i <= T_ROWS:
                     load_row(i)
+            for u in units_of_step.get(step, []):
+                if u + UNITS_AHEAD < N_UNITS:
+                    load_unit(u + UNITS_AHEAD)

@@ -24,6 +24,7 @@ PAIR = 2
 N_PAIRS = T_ROWS // PAIR
 LOADED_AHEAD = 16
 WIDENED_AHEAD = 9
+UNIT_SPAN = 16
 SCALAR_WIDENS_FIRST = (0, 2, 4)
 
 BAND_ROWS = 6
@@ -58,8 +59,7 @@ def tile_graphconvlayer_kernel(tc, X, W_gcn_words, W_gcn_scales, b, H, Wd, out):
         band_pool = ctx.enter_context(tc.tile_pool(name="band", bufs=2))
         mx_pool = ctx.enter_context(tc.tile_pool(name="mx", bufs=3))
         result_pool = ctx.enter_context(tc.tile_pool(name="result", bufs=8))
-        sums_psum = ctx.enter_context(tc.psum_pool(name="sums_psum", bufs=5))
-        prod_psum = ctx.enter_context(tc.psum_pool(name="prod_psum", bufs=3))
+        sums_psum = ctx.enter_context(tc.psum_pool(name="sums_psum", bufs=8))
         ctx.enter_context(tc.manual_schedule())
 
         raw = {}
@@ -98,15 +98,6 @@ def tile_graphconvlayer_kernel(tc, X, W_gcn_words, W_gcn_scales, b, H, Wd, out):
                 above = sums_psum.tile([P, PACK, P], F32, tag="acc")
                 half[-1] = above
             for t in range(PACK):
-                if r < T_ROWS:
-                    nc.tensor.matmul(
-                        out=half[r][:, t, :],
-                        lhsT=wide[r][:, t, :],
-                        rhs=shift_right[:],
-                        is_transpose=True,
-                        start=(t == 0),
-                        stop=False,
-                    )
                 nc.tensor.matmul(
                     out=half[r - 1][:, t, :],
                     lhsT=wide[r][:, t, :],
@@ -115,6 +106,16 @@ def tile_graphconvlayer_kernel(tc, X, W_gcn_words, W_gcn_scales, b, H, Wd, out):
                     start=(r == 0 and t == 0),
                     stop=(t == PACK - 1),
                 )
+            if r < T_ROWS:
+                for t in range(PACK):
+                    nc.tensor.matmul(
+                        out=half[r][:, t, :],
+                        lhsT=wide[r][:, t, :],
+                        rhs=shift_right[:],
+                        is_transpose=True,
+                        start=(t == 0),
+                        stop=False,
+                    )
 
         def keep_half_sums(i):
             in_sbuf = kept_all[:, i + 1, :, :]
@@ -146,7 +147,7 @@ def tile_graphconvlayer_kernel(tc, X, W_gcn_words, W_gcn_scales, b, H, Wd, out):
             scales[pair] = ax_scales
 
         def multiply(key, x_codes, x_scales, cols):
-            prod = prod_psum.tile([P, F_OUT], F32)
+            prod = sums_psum.tile([P, F_OUT], F32, tag="acc")
             nc.tensor.matmul_mx(
                 out=prod[:],
                 lhsT=x_codes[:, cols].bitcast(FP8X4),
@@ -263,8 +264,8 @@ def tile_graphconvlayer_kernel(tc, X, W_gcn_words, W_gcn_scales, b, H, Wd, out):
 
         units_of_step = {}
         for u in range(N_UNITS):
-            units_of_step.setdefault(u * N_PAIRS // N_UNITS, []).append(u)
-        band_done_at = {band: (2 * band + 1) * N_PAIRS // N_UNITS for band in range(len(BANDS))}
+            units_of_step.setdefault(u * UNIT_SPAN // N_UNITS, []).append(u)
+        band_done_at = {band: (2 * band + 1) * UNIT_SPAN // N_UNITS for band in range(len(BANDS))}
         UNITS_AHEAD = 4
 
         for i in range(3):

@@ -11,6 +11,7 @@ I32 = mybir.dt.int32
 FP8X4 = mybir.dt.float8_e4m3fn_x4
 FP4X4 = mybir.dt.float4_e2m1fn_x4
 ADD = mybir.AluOpType.add
+MULT = mybir.AluOpType.mult
 
 P = 128
 PACK = 4
@@ -23,8 +24,13 @@ T_ROWS = 40
 PAIR = 2
 N_PAIRS = T_ROWS // PAIR
 LOADED_AHEAD = 16
-WIDENED_AHEAD = 9
+WIDENED_AHEAD = 5
 UNIT_SPAN = 16
+VECTOR_GROUPS = (0, 1)
+GPSIMD_ADDS = (1, 3, 5, 7)
+GPSIMD_WIDENS = ()
+VECTOR_WIDENS = ()
+QUANTISE_LAG = 1
 SCALAR_WIDENS_FIRST = (0, 2, 4)
 
 BAND_ROWS = 6
@@ -48,18 +54,20 @@ def tile_graphconvlayer_kernel(tc, X, W_gcn_words, W_gcn_scales, b, H, Wd, out):
     x_rows = X.rearrange("b (i j) f -> i j b f", j=GRID)
     x_cols = X.rearrange("b (i j) f -> b j i f", j=GRID)
     x_last_column = X.rearrange("b (i j) f -> j i b f", j=GRID)[GRID - 1]
-    out_rows = out.rearrange("b (i j) n -> i j b n", j=GRID)
+    out_pairs = out.rearrange("b (ij e) n -> ij b (e n)", e=2)
 
     with ExitStack() as ctx:
         const = ctx.enter_context(tc.tile_pool(name="const", bufs=1))
         raw_pool = ctx.enter_context(tc.tile_pool(name="raw", bufs=LOADED_AHEAD))
         window_pool = ctx.enter_context(tc.tile_pool(name="window", bufs=13))
         wide_pool = ctx.enter_context(tc.tile_pool(name="wide", bufs=WIDENED_AHEAD + 3))
-        grouped_pool = ctx.enter_context(tc.tile_pool(name="grouped", bufs=1))
+        grouped_pool = ctx.enter_context(tc.tile_pool(name="grouped", bufs=QUANTISE_LAG))
         band_pool = ctx.enter_context(tc.tile_pool(name="band", bufs=2))
         mx_pool = ctx.enter_context(tc.tile_pool(name="mx", bufs=3))
-        result_pool = ctx.enter_context(tc.tile_pool(name="result", bufs=8))
-        sums_psum = ctx.enter_context(tc.psum_pool(name="sums_psum", bufs=8))
+        result_pool = ctx.enter_context(tc.tile_pool(name="result", bufs=5))
+        sums_psum = ctx.enter_context(tc.psum_pool(name="sums_psum", bufs=3))
+        band_psum = ctx.enter_context(tc.psum_pool(name="band_psum", bufs=1))
+        prod_psum = ctx.enter_context(tc.psum_pool(name="prod_psum", bufs=4))
         ctx.enter_context(tc.manual_schedule())
 
         raw = {}
@@ -85,6 +93,17 @@ def tile_graphconvlayer_kernel(tc, X, W_gcn_words, W_gcn_scales, b, H, Wd, out):
 
         def widen_row(i):
             x_wide = wide_pool.tile([P, PACK, P], F32)
+            if i % 8 in GPSIMD_WIDENS and i >= WIDENED_AHEAD:
+                nc.gpsimd.tensor_scalar(
+                    out=x_wide[:],
+                    in0=raw[i][:].rearrange("c (q t) -> c t q", t=PACK),
+                    scalar1=1.0,
+                    scalar2=0.0,
+                    op0=MULT,
+                    op1=ADD,
+                )
+                wide[i] = x_wide
+                return
             nc.scalar.copy(
                 out=x_wide[:].rearrange("c t q -> c q t"), in_=raw[i][:].rearrange("c (q t) -> c q t", t=PACK)
             )
@@ -101,7 +120,7 @@ def tile_graphconvlayer_kernel(tc, X, W_gcn_words, W_gcn_scales, b, H, Wd, out):
                 nc.tensor.matmul(
                     out=half[r - 1][:, t, :],
                     lhsT=wide[r][:, t, :],
-                    rhs=ident[:],
+                    rhs=ident_eo[:].rearrange("p e jj b -> p (e jj b)"),
                     is_transpose=True,
                     start=(r == 0 and t == 0),
                     stop=(t == PACK - 1),
@@ -111,28 +130,34 @@ def tile_graphconvlayer_kernel(tc, X, W_gcn_words, W_gcn_scales, b, H, Wd, out):
                     nc.tensor.matmul(
                         out=half[r][:, t, :],
                         lhsT=wide[r][:, t, :],
-                        rhs=shift_right[:],
+                        rhs=shift_eo[:].rearrange("p e jj b -> p (e jj b)"),
                         is_transpose=True,
                         start=(t == 0),
                         stop=False,
                     )
 
+        def from_psum(half_sum):
+            return half_sum[:].rearrange("q t (e jj b) -> q e jj b t", e=2, b=BATCH)
+
+        def parity_last(in_row):
+            return in_row.rearrange("q (jj e b) t -> q e jj b t", e=2, b=BATCH)
+
         def keep_half_sums(i):
             in_sbuf = kept_all[:, i + 1, :, :]
-            nc.scalar.copy(out=in_sbuf[:, 0:P, :], in_=half[i][:].rearrange("q t c -> q c t"))
+            nc.scalar.copy(out=parity_last(in_sbuf[:, 0:P, :]), in_=from_psum(half[i]))
             kept[i] = in_sbuf
 
         def neighbour_sum(i):
             if i % PAIR == 0:
-                ax = grouped_pool.tile([P, PAIR, P, PACK], BF16, align_bytes=64)
+                ax = grouped_pool.tile([P, 2, PAIR, P // 2, PACK], BF16, align_bytes=64)
                 grouped[i // PAIR] = ax
-            dst = grouped[i // PAIR][:, i % PAIR, :, :]
-            right_and_above = kept[i - 1][:, BATCH : P + BATCH, :]
-            if i % 2 == 0 or i == T_ROWS - 1:
-                left_and_below = half[i][:].rearrange("q t c -> q c t")
+            dst = grouped[i // PAIR][:, :, i % PAIR, :, :].rearrange("q e (jj b) t -> q e jj b t", b=BATCH)
+            right_and_above = parity_last(kept[i - 1][:, BATCH : P + BATCH, :])
+            if i % 8 not in GPSIMD_ADDS or i == T_ROWS - 1:
+                left_and_below = from_psum(half[i])
                 nc.vector.tensor_tensor(out=dst, in0=left_and_below, in1=right_and_above, op=ADD)
             else:
-                left_and_below = kept[i][:, 0:P, :]
+                left_and_below = parity_last(kept[i][:, 0:P, :])
                 nc.gpsimd.tensor_tensor(out=dst, in0=left_and_below, in1=right_and_above, op=ADD)
 
         def quantise(pair):
@@ -141,13 +166,13 @@ def tile_graphconvlayer_kernel(tc, X, W_gcn_words, W_gcn_scales, b, H, Wd, out):
             nc.vector.quantize_mx(
                 out=ax_codes[:].bitcast(FP8X4),
                 scales=ax_scales[:],
-                in_=grouped[pair][:].rearrange("q r c t -> q (r c t)"),
+                in_=grouped[pair][:].rearrange("q e r c t -> q (e r c t)"),
             )
             codes[pair] = ax_codes
             scales[pair] = ax_scales
 
         def multiply(key, x_codes, x_scales, cols):
-            prod = sums_psum.tile([P, F_OUT], F32, tag="acc")
+            prod = prod_psum.tile([P, F_OUT], F32, tag="acc")
             nc.tensor.matmul_mx(
                 out=prod[:],
                 lhsT=x_codes[:, cols].bitcast(FP8X4),
@@ -159,14 +184,17 @@ def tile_graphconvlayer_kernel(tc, X, W_gcn_words, W_gcn_scales, b, H, Wd, out):
             )
             product[key] = prod
 
-        def multiply_row(i):
-            cols = slice((i % PAIR) * P, (i % PAIR + 1) * P)
-            multiply(i, codes[i // PAIR], scales[i // PAIR], cols)
+        def multiply_pair(pair, e):
+            multiply((pair, e), codes[pair], scales[pair], slice(e * P, (e + 1) * P))
 
-        def add_bias_and_store(key, dst):
-            result = result_pool.tile([P, F_OUT], F32)
-            nc.vector.tensor_tensor(out=result[:], in0=product[key][:], in1=bias[:], op=ADD)
-            nc.sync.dma_start(out=dst, in_=result[:])
+        def add_bias(key, result):
+            nc.vector.tensor_tensor(out=result, in0=product[key][:], in1=bias[:], op=ADD)
+
+        def add_bias_and_store_two(keys, dst):
+            result = result_pool.tile([P, 2, F_OUT], F32)
+            for e in range(2):
+                add_bias(keys[e], result[:, e, :])
+            nc.sync.dma_start(out=dst, in_=result[:].rearrange("p e n -> p (e n)"))
 
         def load_unit(u):
             batch, r0 = BANDS[u // len(UNITS)]
@@ -184,7 +212,7 @@ def tile_graphconvlayer_kernel(tc, X, W_gcn_words, W_gcn_scales, b, H, Wd, out):
             adjacency = adjacency_last if r0 + BAND_ROWS == GRID else adjacency_mid
             unit = UNITS[u % len(UNITS)]
             j0 = WIN_EDGES[unit[0]]
-            acc = sums_psum.tile([P, PACK, 256], BF16, tag="acc")
+            acc = band_psum.tile([P, PACK, 256], BF16, tag="acc")
             for w in unit:
                 j, end = WIN_EDGES[w], WIN_EDGES[w + 1]
                 c = j - WIN_STEP * w
@@ -203,17 +231,25 @@ def tile_graphconvlayer_kernel(tc, X, W_gcn_words, W_gcn_scales, b, H, Wd, out):
             unit = UNITS[u % len(UNITS)]
             j, end = WIN_EDGES[unit[0]], WIN_EDGES[unit[-1] + 1]
             if u % len(UNITS) == 0:
-                ax_band = band_pool.tile([P, BAND_ROWS, GRID, PACK], BF16, align_bytes=64)
+                ax_band = band_pool.tile([P, BAND_TILES * P * PACK], BF16, align_bytes=64)
                 band_ax[band] = ax_band
-            nc.scalar.copy(
-                out=band_ax[band][:, :, j:end, :],
-                in_=acc[:, :, 0 : BAND_ROWS * (end - j)].rearrange("q t (j r) -> q r j t", r=BAND_ROWS),
+            copy = nc.vector.tensor_copy if u in VECTOR_GROUPS else nc.scalar.copy
+            src = acc[:, :, 0 : BAND_ROWS * (end - j)]
+            paired = band_ax[band][:, 0 : 2 * P * PACK].rearrange("q (e r jj t) -> q e r jj t", e=2, r=4, t=PACK)
+            copy(
+                out=paired[:, :, :, j // 2 : end // 2, :],
+                in_=src.rearrange("q t (jj e r) -> q e r jj t", e=2, r=BAND_ROWS)[:, :, 0:4, :, :],
+            )
+            single = band_ax[band][:, 2 * P * PACK :].rearrange("q (r j t) -> q r j t", r=2, t=PACK)
+            copy(
+                out=single[:, :, j:end, :],
+                in_=src.rearrange("q t (j r) -> q r j t", r=BAND_ROWS)[:, 4:6, :, :],
             )
 
         def quantise_band(band):
             band_codes = mx_pool.tile([P, BAND_TILES * P], U32, align_bytes=64)
             band_scales = mx_pool.tile([P, BAND_TILES * P], U8, align_bytes=64)
-            flat = band_ax[band][:].rearrange("q r j t -> q (r j t)")
+            flat = band_ax[band]
             for lo, hi in ((0, 2 * P), (2 * P, 3 * P)):
                 nc.vector.quantize_mx(
                     out=band_codes[:, lo:hi].bitcast(FP8X4),
@@ -226,16 +262,27 @@ def tile_graphconvlayer_kernel(tc, X, W_gcn_words, W_gcn_scales, b, H, Wd, out):
         def multiply_band_tile(band, k):
             multiply(("band", band, k), codes["band", band], scales["band", band], slice(k * P, (k + 1) * P))
 
-        def store_band_tile(band, k):
+        def store_band_tiles(band, ks):
             batch, r0 = BANDS[band]
-            node = (r0 + 2 * k) * GRID
-            add_bias_and_store(("band", band, k), out[batch, node : node + P, :])
+            keys = [("band", band, k) for k in ks]
+            if ks == (0, 1):
+                first_node = r0 * GRID // 2
+                add_bias_and_store_two(keys, out_pairs[first_node : first_node + P, batch, :])
+            else:
+                result = result_pool.tile([P, F_OUT], F32, tag="single")
+                add_bias(keys[0], result[:])
+                node = (r0 + 4) * GRID
+                nc.sync.dma_start(out=out[batch, node : node + P, :], in_=result[:])
 
         ident = const.tile([P, P], F32)
         make_identity(nc, ident[:])
-        shift_right = const.tile([P, P], F32)
-        nc.vector.memset(shift_right[:], 0.0)
-        nc.vector.tensor_copy(out=shift_right[:, BATCH:P], in_=ident[:, 0 : P - BATCH])
+        ident_eo = const.tile([P, 2, GRID // 2, BATCH], F32)
+        shift_eo = const.tile([P, 2, GRID // 2, BATCH], F32)
+        by_parity = ident[:].rearrange("p (jj e b) -> p e jj b", e=2, b=BATCH)
+        nc.vector.memset(shift_eo[:], 0.0)
+        nc.vector.tensor_copy(out=ident_eo[:], in_=by_parity)
+        nc.vector.tensor_copy(out=shift_eo[:, 1, :, :], in_=by_parity[:, 0, :, :])
+        nc.vector.tensor_copy(out=shift_eo[:, 0, 1:, :], in_=by_parity[:, 1, 0 : GRID // 2 - 1, :])
         by_node = ident[:].rearrange("p (c r) -> p c r", r=WIN_ROWS)
         adjacency_mid = const.tile([P, WIN_COLS * BAND_ROWS], BF16)
         adjacency_last = const.tile([P, WIN_COLS * BAND_ROWS], BF16)
@@ -308,24 +355,28 @@ def tile_graphconvlayer_kernel(tc, X, W_gcn_words, W_gcn_scales, b, H, Wd, out):
         )
         keep_half_sums(-1)
 
-        for step in range(N_PAIRS + 2):
+        for step in range(N_PAIRS + QUANTISE_LAG + 1):
             first = PAIR * step
-            done = first - 2 * PAIR
-            band_tiles = [(band, k) for band, at in band_done_at.items() for k in range(BAND_TILES) if at + 2 + k // 2 == step]
+            done = first - PAIR * (QUANTISE_LAG + 1)
+            band_tiles = [(band, ks) for band, at in band_done_at.items() for ks in ((0, 1), (2,)) if at + 2 + ks[0] // 2 == step]
             if step < N_PAIRS:
                 transpose_row(first + 1)
                 transpose_row(first + 2)
             accs = [(u, gather_unit(u)) for u in units_of_step.get(step, [])]
             if done >= 0:
-                multiply_row(done)
-                multiply_row(done + 1)
-            for band, k in band_tiles:
-                multiply_band_tile(band, k)
+                multiply_pair(done // PAIR, 0)
+                multiply_pair(done // PAIR, 1)
+            for band, ks in band_tiles:
+                for k in ks:
+                    multiply_band_tile(band, k)
             for band, at in band_done_at.items():
                 if at + 1 == step:
                     quantise_band(band)
-            if 0 <= step - 1 < N_PAIRS:
-                quantise(step - 1)
+            if 0 <= step - QUANTISE_LAG < N_PAIRS:
+                quantise(step - QUANTISE_LAG)
+            for i in (first + WIDENED_AHEAD, first + WIDENED_AHEAD + 1):
+                if i <= T_ROWS and i % 8 in VECTOR_WIDENS:
+                    widen_row_on_vector(i)
             if step < N_PAIRS:
                 keep_half_sums(first)
                 if first + 1 < T_ROWS - 1:
@@ -336,12 +387,12 @@ def tile_graphconvlayer_kernel(tc, X, W_gcn_words, W_gcn_scales, b, H, Wd, out):
                 neighbour_sum(first)
                 neighbour_sum(first + 1)
             if done >= 0:
-                add_bias_and_store(done, out_rows[done])
-                add_bias_and_store(done + 1, out_rows[done + 1])
-            for band, k in band_tiles:
-                store_band_tile(band, k)
+                keys = [(done // PAIR, 0), (done // PAIR, 1)]
+                add_bias_and_store_two(keys, out_pairs[done * GRID // 2 : (done + PAIR) * GRID // 2, :, :])
+            for band, ks in band_tiles:
+                store_band_tiles(band, ks)
             for i in (first + WIDENED_AHEAD, first + WIDENED_AHEAD + 1):
-                if i <= T_ROWS:
+                if i <= T_ROWS and i % 8 not in VECTOR_WIDENS:
                     widen_row(i)
             for i in (first + LOADED_AHEAD, first + LOADED_AHEAD + 1):
                 if i <= T_ROWS:

@@ -26,11 +26,11 @@ N_PAIRS = T_ROWS // PAIR
 LOADED_AHEAD = 16
 WIDENED_AHEAD = 5
 UNIT_SPAN = 16
-VECTOR_GROUPS = (0, 1)
-GPSIMD_ADDS = (1, 3, 5, 7)
+VECTOR_GROUPS = tuple(range(0, 16, 2))
+GPSIMD_ADDS = (0, 1, 2, 3, 4, 5, 6, 7)
 GPSIMD_WIDENS = ()
 VECTOR_WIDENS = ()
-QUANTISE_LAG = 1
+QUANTISE_LAG = 2
 SCALAR_WIDENS_FIRST = (0, 2, 4)
 
 BAND_ROWS = 6

@@ -184,6 +184,11 @@ def tile_graphconvlayer_kernel(tc, X, W_gcn_words, W_gcn_scales, b, H, Wd, out):
             )
             product[key] = prod
 
+        def spread_bias():
+            bias_sum = prod_psum.tile([P, F_OUT], F32, tag="acc")
+            nc.tensor.matmul(out=bias_sum[:], lhsT=ones[:], rhs=bias_row[:], start=True, stop=True)
+            nc.vector.tensor_copy(out=bias[:], in_=bias_sum[:])
+
         def multiply_pair(pair, e):
             multiply((pair, e), codes[pair], scales[pair], slice(e * P, (e + 1) * P))
 
@@ -194,7 +199,10 @@ def tile_graphconvlayer_kernel(tc, X, W_gcn_words, W_gcn_scales, b, H, Wd, out):
             result = result_pool.tile([P, 2, F_OUT], F32)
             for e in range(2):
                 add_bias(keys[e], result[:, e, :])
-            nc.sync.dma_start(out=dst, in_=result[:].rearrange("p e n -> p (e n)"))
+                if keys[0] == (N_PAIRS - 1, 0):
+                    nc.sync.dma_start(out=dst[:, :, e * F_OUT : (e + 1) * F_OUT], in_=result[:, e, :])
+            if keys[0] != (N_PAIRS - 1, 0):
+                nc.sync.dma_start(out=dst, in_=result[:].rearrange("p e n -> p (e n)"))
 
         def load_unit(u):
             batch, r0 = BANDS[u // len(UNITS)]
@@ -299,15 +307,17 @@ def tile_graphconvlayer_kernel(tc, X, W_gcn_words, W_gcn_scales, b, H, Wd, out):
             ):
                 nc.vector.tensor_tensor(out=out_part, in0=out_part, in1=in_part, op=ADD)
 
-        build_adjacency(adjacency_mid, 1)
-        build_adjacency(adjacency_last, 2)
         kept_all = const.tile([P, T_ROWS, P + BATCH, PACK], F32)
         last_column = const.tile([P, P + BATCH, PACK], F32)
-        nc.vector.memset(last_column[:], 0.0)
+        nc.gpsimd.memset(last_column[:], 0.0)
         w_scales = const.tile([P, F_OUT], U8, align_bytes=64)
         nc.vector.memset(w_scales[:].bitcast(I32), 0)
         w_words = const.tile([P, 2 * F_OUT], U8, align_bytes=64)
         bias = const.tile([P, F_OUT], BF16)
+        bias_row = const.tile([P, F_OUT], BF16)
+        nc.gpsimd.memset(bias_row[:], 0.0)
+        ones = const.tile([P, P], BF16)
+        nc.gpsimd.memset(ones[:], 1.0)
 
         units_of_step = {}
         for u in range(N_UNITS):
@@ -315,10 +325,10 @@ def tile_graphconvlayer_kernel(tc, X, W_gcn_words, W_gcn_scales, b, H, Wd, out):
         band_done_at = {band: (2 * band + 1) * UNIT_SPAN // N_UNITS for band in range(len(BANDS))}
         UNITS_AHEAD = 4
 
-        for i in range(3):
-            load_row(i)
         edge_raw = const.tile([P, F_IN], BF16)
         nc.sync.dma_start(out=edge_raw[:], in_=x_last_column)
+        for i in range(3):
+            load_row(i)
         for i in range(3, 5):
             load_row(i)
         load_unit(0)
@@ -330,30 +340,31 @@ def tile_graphconvlayer_kernel(tc, X, W_gcn_words, W_gcn_scales, b, H, Wd, out):
                 out=w_scales[32 * quadrant : 32 * quadrant + 4, :].bitcast(I32),
                 in_=W_gcn_scales[0, 4 * quadrant : 4 * quadrant + 4, :].bitcast(I32),
             )
+        nc.sync.dma_start(out=bias_row[0:1, :], in_=b.unsqueeze(0))
         for u in range(1, UNITS_AHEAD):
             load_unit(u)
         for i in range(WIDENED_AHEAD, LOADED_AHEAD):
             load_row(i)
 
         edge_wide = const.tile([P, PACK, P], F32)
-        for i in range(WIDENED_AHEAD):
-            if i in SCALAR_WIDENS_FIRST:
-                widen_row(i)
-            else:
-                widen_row_on_vector(i)
-            if i == 1:
-                nc.vector.tensor_copy(out=edge_wide[:], in_=edge_raw[:].rearrange("c (q t) -> c t q", t=PACK))
-        nc.scalar.dma_start(out=bias[:], in_=b.partition_broadcast(P))
-        transpose_row(0)
-        edge_t = sums_psum.tile([P, PACK, P], F32, tag="acc")
+        nc.vector.tensor_copy(out=edge_wide[:], in_=edge_raw[:].rearrange("c (q t) -> c t q", t=PACK))
+        widen_row(0)
+        widen_row_on_vector(1)
+        widen_row(2)
+        edge_t = prod_psum.tile([P, PACK, P], F32, tag="acc")
         for t in range(PACK):
             nc.tensor.transpose(edge_t[:, t, :], edge_wide[:, t, :], ident[:])
+        transpose_row(0)
         nc.vector.tensor_copy(out=last_column[:, BATCH : P + BATCH, :], in_=edge_t[:].rearrange("q t c -> q c t"))
         nc.vector.tensor_copy(
             out=kept_all[:, :, P : P + BATCH, :],
             in_=last_column[:, 0 : BATCH * T_ROWS, :].rearrange("q (i b) t -> q i b t", b=BATCH),
         )
         keep_half_sums(-1)
+        widen_row_on_vector(3)
+        build_adjacency(adjacency_mid, 1)
+        widen_row(4)
+        build_adjacency(adjacency_last, 2)
 
         for step in range(N_PAIRS + QUANTISE_LAG + 1):
             first = PAIR * step
@@ -391,6 +402,8 @@ def tile_graphconvlayer_kernel(tc, X, W_gcn_words, W_gcn_scales, b, H, Wd, out):
                 add_bias_and_store_two(keys, out_pairs[done * GRID // 2 : (done + PAIR) * GRID // 2, :, :])
             for band, ks in band_tiles:
                 store_band_tiles(band, ks)
+            if step == 0:
+                spread_bias()
             for i in (first + WIDENED_AHEAD, first + WIDENED_AHEAD + 1):
                 if i <= T_ROWS and i % 8 not in VECTOR_WIDENS:
                     widen_row(i)

@@ -23,10 +23,10 @@ F_OUT = 512
 T_ROWS = 40
 PAIR = 2
 N_PAIRS = T_ROWS // PAIR
-LOADED_AHEAD = 16
+STEPS_AHEAD = 5
 WIDENED_AHEAD = 5
 UNIT_SPAN = 16
-VECTOR_GROUPS = tuple(range(0, 16, 2))
+VECTOR_GROUPS = (0, 1, 2, 4, 8, 12)
 GPSIMD_ADDS = (0, 1, 2, 3, 4, 5, 6, 7)
 GPSIMD_WIDENS = ()
 VECTOR_WIDENS = ()
@@ -58,8 +58,8 @@ def tile_graphconvlayer_kernel(tc, X, W_gcn_words, W_gcn_scales, b, H, Wd, out):
 
     with ExitStack() as ctx:
         const = ctx.enter_context(tc.tile_pool(name="const", bufs=1))
-        raw_pool = ctx.enter_context(tc.tile_pool(name="raw", bufs=LOADED_AHEAD))
-        window_pool = ctx.enter_context(tc.tile_pool(name="window", bufs=13))
+        raw_pool = ctx.enter_context(tc.tile_pool(name="raw", bufs=WIDENED_AHEAD + PAIR * STEPS_AHEAD))
+        window_pool = ctx.enter_context(tc.tile_pool(name="window", bufs=5 * (STEPS_AHEAD + 2) // 2))
         wide_pool = ctx.enter_context(tc.tile_pool(name="wide", bufs=WIDENED_AHEAD + 3))
         grouped_pool = ctx.enter_context(tc.tile_pool(name="grouped", bufs=QUANTISE_LAG))
         band_pool = ctx.enter_context(tc.tile_pool(name="band", bufs=2))
@@ -323,17 +323,20 @@ def tile_graphconvlayer_kernel(tc, X, W_gcn_words, W_gcn_scales, b, H, Wd, out):
         for u in range(N_UNITS):
             units_of_step.setdefault(u * UNIT_SPAN // N_UNITS, []).append(u)
         band_done_at = {band: (2 * band + 1) * UNIT_SPAN // N_UNITS for band in range(len(BANDS))}
-        UNITS_AHEAD = 4
+
+        def load_for_step(step):
+            for i in (PAIR * step + WIDENED_AHEAD, PAIR * step + WIDENED_AHEAD + 1):
+                if i <= T_ROWS:
+                    load_row(i)
+            for u in units_of_step.get(step + 1, []):
+                load_unit(u)
 
         edge_raw = const.tile([P, F_IN], BF16)
         nc.sync.dma_start(out=edge_raw[:], in_=x_last_column)
-        for i in range(3):
-            load_row(i)
-        for i in range(3, 5):
+        for i in range(WIDENED_AHEAD):
             load_row(i)
         load_unit(0)
-        for i in range(5, WIDENED_AHEAD):
-            load_row(i)
+        load_for_step(0)
         nc.sync.dma_start(out=w_words[:].bitcast(I32), in_=W_gcn_words[0].bitcast(I32))
         for quadrant in range(4):
             nc.sync.dma_start(
@@ -341,10 +344,8 @@ def tile_graphconvlayer_kernel(tc, X, W_gcn_words, W_gcn_scales, b, H, Wd, out):
                 in_=W_gcn_scales[0, 4 * quadrant : 4 * quadrant + 4, :].bitcast(I32),
             )
         nc.sync.dma_start(out=bias_row[0:1, :], in_=b.unsqueeze(0))
-        for u in range(1, UNITS_AHEAD):
-            load_unit(u)
-        for i in range(WIDENED_AHEAD, LOADED_AHEAD):
-            load_row(i)
+        for step in range(1, STEPS_AHEAD):
+            load_for_step(step)
 
         edge_wide = const.tile([P, PACK, P], F32)
         nc.vector.tensor_copy(out=edge_wide[:], in_=edge_raw[:].rearrange("c (q t) -> c t q", t=PACK))
@@ -407,9 +408,4 @@ def tile_graphconvlayer_kernel(tc, X, W_gcn_words, W_gcn_scales, b, H, Wd, out):
             for i in (first + WIDENED_AHEAD, first + WIDENED_AHEAD + 1):
                 if i <= T_ROWS and i % 8 not in VECTOR_WIDENS:
                     widen_row(i)
-            for i in (first + LOADED_AHEAD, first + LOADED_AHEAD + 1):
-                if i <= T_ROWS:
-                    load_row(i)
-            for u in units_of_step.get(step, []):
-                if u + UNITS_AHEAD < N_UNITS:
-                    load_unit(u + UNITS_AHEAD)
+            load_for_step(step + STEPS_AHEAD)

@@ -337,6 +337,7 @@ def tile_graphconvlayer_kernel(tc, X, W_gcn_words, W_gcn_scales, b, H, Wd, out):
             load_row(i)
         load_unit(0)
         load_for_step(0)
+        load_for_step(1)
         nc.sync.dma_start(out=w_words[:].bitcast(I32), in_=W_gcn_words[0].bitcast(I32))
         for quadrant in range(4):
             nc.sync.dma_start(
@@ -344,7 +345,7 @@ def tile_graphconvlayer_kernel(tc, X, W_gcn_words, W_gcn_scales, b, H, Wd, out):
                 in_=W_gcn_scales[0, 4 * quadrant : 4 * quadrant + 4, :].bitcast(I32),
             )
         nc.sync.dma_start(out=bias_row[0:1, :], in_=b.unsqueeze(0))
-        for step in range(1, STEPS_AHEAD):
+        for step in range(2, STEPS_AHEAD):
             load_for_step(step)
 
         edge_wide = const.tile([P, PACK, P], F32)
@@ -403,7 +404,7 @@ def tile_graphconvlayer_kernel(tc, X, W_gcn_words, W_gcn_scales, b, H, Wd, out):
                 add_bias_and_store_two(keys, out_pairs[done * GRID // 2 : (done + PAIR) * GRID // 2, :, :])
             for band, ks in band_tiles:
                 store_band_tiles(band, ks)
-            if step == 0:
+            if step == 2:
                 spread_bias()
             for i in (first + WIDENED_AHEAD, first + WIDENED_AHEAD + 1):
                 if i <= T_ROWS and i % 8 not in VECTOR_WIDENS:

from contextlib import ExitStack

import concourse.mybir as mybir
from concourse.masks import make_identity

F32 = mybir.dt.float32
BF16 = mybir.dt.bfloat16
U8 = mybir.dt.uint8
U32 = mybir.dt.uint32
I32 = mybir.dt.int32
FP8X4 = mybir.dt.float8_e4m3fn_x4
FP4X4 = mybir.dt.float4_e2m1fn_x4
ADD = mybir.AluOpType.add
MULT = mybir.AluOpType.mult

P = 128
PACK = 4
BATCH = 2
GRID = 64
F_IN = 512
F_OUT = 512

T_ROWS = 40
PAIR = 2
N_PAIRS = T_ROWS // PAIR
STEPS_AHEAD = 5
WIDENED_AHEAD = 5
UNIT_SPAN = 16
VECTOR_GROUPS = (0, 1, 2, 4, 8, 12)
GPSIMD_ADDS = (0, 1, 2, 3, 4, 5, 6, 7)
GPSIMD_WIDENS = ()
VECTOR_WIDENS = ()
QUANTISE_LAG = 2
SCALAR_WIDENS_FIRST = (0, 2, 4)

BAND_ROWS = 6
WIN_ROWS = 8
WIN_COLS = 16
WIN_STEP = 12
WIN_EDGES = (0, 14, 26, 38, 50, 64)
UNITS = ((0, 1, 2), (3, 4))
BANDS = tuple((b, r0) for r0 in range(T_ROWS, GRID, BAND_ROWS) for b in range(BATCH))
N_UNITS = len(BANDS) * len(UNITS)
BAND_TILES = BAND_ROWS * GRID // P

FLOPS = 2 * BATCH * GRID * GRID * F_IN * F_OUT


def tile_graphconvlayer_kernel(tc, X, W_gcn_words, W_gcn_scales, b, H, Wd, out):
    nc = tc.nc
    assert (H, Wd) == (GRID, GRID)
    assert BATCH * GRID == P and PACK * P == F_IN

    x_rows = X.rearrange("b (i j) f -> i j b f", j=GRID)
    x_cols = X.rearrange("b (i j) f -> b j i f", j=GRID)
    x_last_column = X.rearrange("b (i j) f -> j i b f", j=GRID)[GRID - 1]
    out_pairs = out.rearrange("b (ij e) n -> ij b (e n)", e=2)

    with ExitStack() as ctx:
        const = ctx.enter_context(tc.tile_pool(name="const", bufs=1))
        raw_pool = ctx.enter_context(tc.tile_pool(name="raw", bufs=WIDENED_AHEAD + PAIR * STEPS_AHEAD))
        window_pool = ctx.enter_context(tc.tile_pool(name="window", bufs=5 * (STEPS_AHEAD + 2) // 2))
        wide_pool = ctx.enter_context(tc.tile_pool(name="wide", bufs=WIDENED_AHEAD + 3))
        grouped_pool = ctx.enter_context(tc.tile_pool(name="grouped", bufs=QUANTISE_LAG))
        band_pool = ctx.enter_context(tc.tile_pool(name="band", bufs=2))
        mx_pool = ctx.enter_context(tc.tile_pool(name="mx", bufs=3))
        result_pool = ctx.enter_context(tc.tile_pool(name="result", bufs=5))
        sums_psum = ctx.enter_context(tc.psum_pool(name="sums_psum", bufs=3))
        band_psum = ctx.enter_context(tc.psum_pool(name="band_psum", bufs=1))
        prod_psum = ctx.enter_context(tc.psum_pool(name="prod_psum", bufs=4))
        ctx.enter_context(tc.manual_schedule())

        raw = {}
        wide = {}
        half = {}
        kept = {}
        grouped = {}
        codes = {}
        scales = {}
        product = {}
        windows = {}
        band_ax = {}

        def load_row(i):
            x_raw = raw_pool.tile([P, F_IN], BF16)
            nc.sync.dma_start(out=x_raw[:], in_=x_rows[i])
            raw[i] = x_raw

        def widen_row_on_vector(i):
            x_wide = wide_pool.tile([P, PACK, P], F32)
            nc.vector.tensor_copy(out=x_wide[:], in_=raw[i][:].rearrange("c (q t) -> c t q", t=PACK))
            wide[i] = x_wide

        def widen_row(i):
            x_wide = wide_pool.tile([P, PACK, P], F32)
            if i % 8 in GPSIMD_WIDENS and i >= WIDENED_AHEAD:
                nc.gpsimd.tensor_scalar(
                    out=x_wide[:],
                    in0=raw[i][:].rearrange("c (q t) -> c t q", t=PACK),
                    scalar1=1.0,
                    scalar2=0.0,
                    op0=MULT,
                    op1=ADD,
                )
                wide[i] = x_wide
                return
            nc.scalar.copy(
                out=x_wide[:].rearrange("c t q -> c q t"), in_=raw[i][:].rearrange("c (q t) -> c q t", t=PACK)
            )
            wide[i] = x_wide

        def transpose_row(r):
            if r < T_ROWS:
                acc = sums_psum.tile([P, PACK, P], F32, tag="acc")
                half[r] = acc
            if r == 0:
                above = sums_psum.tile([P, PACK, P], F32, tag="acc")
                half[-1] = above
            for t in range(PACK):
                nc.tensor.matmul(
                    out=half[r - 1][:, t, :],
                    lhsT=wide[r][:, t, :],
                    rhs=ident_eo[:].rearrange("p e jj b -> p (e jj b)"),
                    is_transpose=True,
                    start=(r == 0 and t == 0),
                    stop=(t == PACK - 1),
                )
            if r < T_ROWS:
                for t in range(PACK):
                    nc.tensor.matmul(
                        out=half[r][:, t, :],
                        lhsT=wide[r][:, t, :],
                        rhs=shift_eo[:].rearrange("p e jj b -> p (e jj b)"),
                        is_transpose=True,
                        start=(t == 0),
                        stop=False,
                    )

        def from_psum(half_sum):
            return half_sum[:].rearrange("q t (e jj b) -> q e jj b t", e=2, b=BATCH)

        def parity_last(in_row):
            return in_row.rearrange("q (jj e b) t -> q e jj b t", e=2, b=BATCH)

        def keep_half_sums(i):
            in_sbuf = kept_all[:, i + 1, :, :]
            nc.scalar.copy(out=parity_last(in_sbuf[:, 0:P, :]), in_=from_psum(half[i]))
            kept[i] = in_sbuf

        def neighbour_sum(i):
            if i % PAIR == 0:
                ax = grouped_pool.tile([P, 2, PAIR, P // 2, PACK], BF16, align_bytes=64)
                grouped[i // PAIR] = ax
            dst = grouped[i // PAIR][:, :, i % PAIR, :, :].rearrange("q e (jj b) t -> q e jj b t", b=BATCH)
            right_and_above = parity_last(kept[i - 1][:, BATCH : P + BATCH, :])
            if i % 8 not in GPSIMD_ADDS or i == T_ROWS - 1:
                left_and_below = from_psum(half[i])
                nc.vector.tensor_tensor(out=dst, in0=left_and_below, in1=right_and_above, op=ADD)
            else:
                left_and_below = parity_last(kept[i][:, 0:P, :])
                nc.gpsimd.tensor_tensor(out=dst, in0=left_and_below, in1=right_and_above, op=ADD)

        def quantise(pair):
            ax_codes = mx_pool.tile([P, PAIR * P], U32, align_bytes=64)
            ax_scales = mx_pool.tile([P, PAIR * P], U8, align_bytes=64)
            nc.vector.quantize_mx(
                out=ax_codes[:].bitcast(FP8X4),
                scales=ax_scales[:],
                in_=grouped[pair][:].rearrange("q e r c t -> q (e r c t)"),
            )
            codes[pair] = ax_codes
            scales[pair] = ax_scales

        def multiply(key, x_codes, x_scales, cols):
            prod = prod_psum.tile([P, F_OUT], F32, tag="acc")
            nc.tensor.matmul_mx(
                out=prod[:],
                lhsT=x_codes[:, cols].bitcast(FP8X4),
                lhsT_scale=x_scales[:, cols],
                rhs=w_words[:].bitcast(FP4X4),
                rhs_scale=w_scales[:],
                start=True,
                stop=True,
            )
            product[key] = prod

        def spread_bias():
            bias_sum = prod_psum.tile([P, F_OUT], F32, tag="acc")
            nc.tensor.matmul(out=bias_sum[:], lhsT=ones[:], rhs=bias_row[:], start=True, stop=True)
            nc.vector.tensor_copy(out=bias[:], in_=bias_sum[:])

        def multiply_pair(pair, e):
            multiply((pair, e), codes[pair], scales[pair], slice(e * P, (e + 1) * P))

        def add_bias(key, result):
            nc.vector.tensor_tensor(out=result, in0=product[key][:], in1=bias[:], op=ADD)

        def add_bias_and_store_two(keys, dst):
            result = result_pool.tile([P, 2, F_OUT], F32)
            for e in range(2):
                add_bias(keys[e], result[:, e, :])
                if keys[0] == (N_PAIRS - 1, 0):
                    nc.sync.dma_start(out=dst[:, :, e * F_OUT : (e + 1) * F_OUT], in_=result[:, e, :])
            if keys[0] != (N_PAIRS - 1, 0):
                nc.sync.dma_start(out=dst, in_=result[:].rearrange("p e n -> p (e n)"))

        def load_unit(u):
            batch, r0 = BANDS[u // len(UNITS)]
            first_row = min(r0 - 1, GRID - WIN_ROWS)
            for w in UNITS[u % len(UNITS)]:
                x_win = window_pool.tile([P, F_IN], BF16)
                nc.sync.dma_start(
                    out=x_win[:],
                    in_=x_cols[batch, WIN_STEP * w : WIN_STEP * w + WIN_COLS, first_row : first_row + WIN_ROWS, :],
                )
                windows[u, w] = x_win

        def gather_unit(u):
            batch, r0 = BANDS[u // len(UNITS)]
            adjacency = adjacency_last if r0 + BAND_ROWS == GRID else adjacency_mid
            unit = UNITS[u % len(UNITS)]
            j0 = WIN_EDGES[unit[0]]
            acc = band_psum.tile([P, PACK, 256], BF16, tag="acc")
            for w in unit:
                j, end = WIN_EDGES[w], WIN_EDGES[w + 1]
                c = j - WIN_STEP * w
                for t in range(PACK):
                    nc.tensor.matmul(
                        out=acc[:, t, BAND_ROWS * (j - j0) : BAND_ROWS * (end - j0)],
                        lhsT=windows[u, w][:].rearrange("p (q t) -> p t q", t=PACK)[:, t, :],
                        rhs=adjacency[:, BAND_ROWS * c : BAND_ROWS * (c + end - j)],
                        start=True,
                        stop=True,
                    )
            return acc

        def group_unit(u, acc):
            band = u // len(UNITS)
            unit = UNITS[u % len(UNITS)]
            j, end = WIN_EDGES[unit[0]], WIN_EDGES[unit[-1] + 1]
            if u % len(UNITS) == 0:
                ax_band = band_pool.tile([P, BAND_TILES * P * PACK], BF16, align_bytes=64)
                band_ax[band] = ax_band
            copy = nc.vector.tensor_copy if u in VECTOR_GROUPS else nc.scalar.copy
            src = acc[:, :, 0 : BAND_ROWS * (end - j)]
            paired = band_ax[band][:, 0 : 2 * P * PACK].rearrange("q (e r jj t) -> q e r jj t", e=2, r=4, t=PACK)
            copy(
                out=paired[:, :, :, j // 2 : end // 2, :],
                in_=src.rearrange("q t (jj e r) -> q e r jj t", e=2, r=BAND_ROWS)[:, :, 0:4, :, :],
            )
            single = band_ax[band][:, 2 * P * PACK :].rearrange("q (r j t) -> q r j t", r=2, t=PACK)
            copy(
                out=single[:, :, j:end, :],
                in_=src.rearrange("q t (j r) -> q r j t", r=BAND_ROWS)[:, 4:6, :, :],
            )

        def quantise_band(band):
            band_codes = mx_pool.tile([P, BAND_TILES * P], U32, align_bytes=64)
            band_scales = mx_pool.tile([P, BAND_TILES * P], U8, align_bytes=64)
            flat = band_ax[band]
            for lo, hi in ((0, 2 * P), (2 * P, 3 * P)):
                nc.vector.quantize_mx(
                    out=band_codes[:, lo:hi].bitcast(FP8X4),
                    scales=band_scales[:, lo:hi],
                    in_=flat[:, PACK * lo : PACK * hi],
                )
            codes["band", band] = band_codes
            scales["band", band] = band_scales

        def multiply_band_tile(band, k):
            multiply(("band", band, k), codes["band", band], scales["band", band], slice(k * P, (k + 1) * P))

        def store_band_tiles(band, ks):
            batch, r0 = BANDS[band]
            keys = [("band", band, k) for k in ks]
            if ks == (0, 1):
                first_node = r0 * GRID // 2
                add_bias_and_store_two(keys, out_pairs[first_node : first_node + P, batch, :])
            else:
                result = result_pool.tile([P, F_OUT], F32, tag="single")
                add_bias(keys[0], result[:])
                node = (r0 + 4) * GRID
                nc.sync.dma_start(out=out[batch, node : node + P, :], in_=result[:])

        ident = const.tile([P, P], F32)
        make_identity(nc, ident[:])
        ident_eo = const.tile([P, 2, GRID // 2, BATCH], F32)
        shift_eo = const.tile([P, 2, GRID // 2, BATCH], F32)
        by_parity = ident[:].rearrange("p (jj e b) -> p e jj b", e=2, b=BATCH)
        nc.vector.memset(shift_eo[:], 0.0)
        nc.vector.tensor_copy(out=ident_eo[:], in_=by_parity)
        nc.vector.tensor_copy(out=shift_eo[:, 1, :, :], in_=by_parity[:, 0, :, :])
        nc.vector.tensor_copy(out=shift_eo[:, 0, 1:, :], in_=by_parity[:, 1, 0 : GRID // 2 - 1, :])
        by_node = ident[:].rearrange("p (c r) -> p c r", r=WIN_ROWS)
        adjacency_mid = const.tile([P, WIN_COLS * BAND_ROWS], BF16)
        adjacency_last = const.tile([P, WIN_COLS * BAND_ROWS], BF16)

        def build_adjacency(adjacency, r0):
            a = adjacency[:].rearrange("p (c r) -> p c r", r=BAND_ROWS)
            nc.vector.tensor_copy(out=a, in_=by_node[:, :, r0 - 1 : r0 - 1 + BAND_ROWS])
            below = min(BAND_ROWS, WIN_ROWS - 1 - r0)
            here = slice(r0, r0 + BAND_ROWS)
            for out_part, in_part in (
                (a[:, :, 0:below], by_node[:, :, r0 + 1 : r0 + 1 + below]),
                (a[:, 1:WIN_COLS, :], by_node[:, 0 : WIN_COLS - 1, here]),
                (a[:, 0 : WIN_COLS - 1, :], by_node[:, 1:WIN_COLS, here]),
            ):
                nc.vector.tensor_tensor(out=out_part, in0=out_part, in1=in_part, op=ADD)

        kept_all = const.tile([P, T_ROWS, P + BATCH, PACK], F32)
        last_column = const.tile([P, P + BATCH, PACK], F32)
        nc.gpsimd.memset(last_column[:], 0.0)
        w_scales = const.tile([P, F_OUT], U8, align_bytes=64)
        nc.vector.memset(w_scales[:].bitcast(I32), 0)
        w_words = const.tile([P, 2 * F_OUT], U8, align_bytes=64)
        bias = const.tile([P, F_OUT], BF16)
        bias_row = const.tile([P, F_OUT], BF16)
        nc.gpsimd.memset(bias_row[:], 0.0)
        ones = const.tile([P, P], BF16)
        nc.gpsimd.memset(ones[:], 1.0)

        units_of_step = {}
        for u in range(N_UNITS):
            units_of_step.setdefault(u * UNIT_SPAN // N_UNITS, []).append(u)
        band_done_at = {band: (2 * band + 1) * UNIT_SPAN // N_UNITS for band in range(len(BANDS))}

        def load_for_step(step):
            for i in (PAIR * step + WIDENED_AHEAD, PAIR * step + WIDENED_AHEAD + 1):
                if i <= T_ROWS:
                    load_row(i)
            for u in units_of_step.get(step + 1, []):
                load_unit(u)

        edge_raw = const.tile([P, F_IN], BF16)
        nc.sync.dma_start(out=edge_raw[:], in_=x_last_column)
        for i in range(WIDENED_AHEAD):
            load_row(i)
        load_unit(0)
        load_for_step(0)
        load_for_step(1)
        nc.sync.dma_start(out=w_words[:].bitcast(I32), in_=W_gcn_words[0].bitcast(I32))
        for quadrant in range(4):
            nc.sync.dma_start(
                out=w_scales[32 * quadrant : 32 * quadrant + 4, :].bitcast(I32),
                in_=W_gcn_scales[0, 4 * quadrant : 4 * quadrant + 4, :].bitcast(I32),
            )
        nc.sync.dma_start(out=bias_row[0:1, :], in_=b.unsqueeze(0))
        for step in range(2, STEPS_AHEAD):
            load_for_step(step)

        edge_wide = const.tile([P, PACK, P], F32)
        nc.vector.tensor_copy(out=edge_wide[:], in_=edge_raw[:].rearrange("c (q t) -> c t q", t=PACK))
        widen_row(0)
        widen_row_on_vector(1)
        widen_row(2)
        edge_t = prod_psum.tile([P, PACK, P], F32, tag="acc")
        for t in range(PACK):
            nc.tensor.transpose(edge_t[:, t, :], edge_wide[:, t, :], ident[:])
        transpose_row(0)
        nc.vector.tensor_copy(out=last_column[:, BATCH : P + BATCH, :], in_=edge_t[:].rearrange("q t c -> q c t"))
        nc.vector.tensor_copy(
            out=kept_all[:, :, P : P + BATCH, :],
            in_=last_column[:, 0 : BATCH * T_ROWS, :].rearrange("q (i b) t -> q i b t", b=BATCH),
        )
        keep_half_sums(-1)
        widen_row_on_vector(3)
        build_adjacency(adjacency_mid, 1)
        widen_row(4)
        build_adjacency(adjacency_last, 2)

        for step in range(N_PAIRS + QUANTISE_LAG + 1):
            first = PAIR * step
            done = first - PAIR * (QUANTISE_LAG + 1)
            band_tiles = [(band, ks) for band, at in band_done_at.items() for ks in ((0, 1), (2,)) if at + 2 + ks[0] // 2 == step]
            if step < N_PAIRS:
                transpose_row(first + 1)
                transpose_row(first + 2)
            accs = [(u, gather_unit(u)) for u in units_of_step.get(step, [])]
            if done >= 0:
                multiply_pair(done // PAIR, 0)
                multiply_pair(done // PAIR, 1)
            for band, ks in band_tiles:
                for k in ks:
                    multiply_band_tile(band, k)
            for band, at in band_done_at.items():
                if at + 1 == step:
                    quantise_band(band)
            if 0 <= step - QUANTISE_LAG < N_PAIRS:
                quantise(step - QUANTISE_LAG)
            for i in (first + WIDENED_AHEAD, first + WIDENED_AHEAD + 1):
                if i <= T_ROWS and i % 8 in VECTOR_WIDENS:
                    widen_row_on_vector(i)
            if step < N_PAIRS:
                keep_half_sums(first)
                if first + 1 < T_ROWS - 1:
                    keep_half_sums(first + 1)
            for u, acc in accs:
                group_unit(u, acc)
            if step < N_PAIRS:
                neighbour_sum(first)
                neighbour_sum(first + 1)
            if done >= 0:
                keys = [(done // PAIR, 0), (done // PAIR, 1)]
                add_bias_and_store_two(keys, out_pairs[done * GRID // 2 : (done + PAIR) * GRID // 2, :, :])
            for band, ks in band_tiles:
                store_band_tiles(band, ks)
            if step == 2:
                spread_bias()
            for i in (first + WIDENED_AHEAD, first + WIDENED_AHEAD + 1):
                if i <= T_ROWS and i % 8 not in VECTOR_WIDENS:
                    widen_row(i)
            load_for_step(step + STEPS_AHEAD)
